import numpy as np
import ml_dtypes


def mxq(x, axis, fmt="e4m3"):
    dtype, down = {"e4m3": (ml_dtypes.float8_e4m3fn, 7), "e5m2": (ml_dtypes.float8_e5m2, 14)}[fmt]
    v = np.moveaxis(np.asarray(x, np.float32).astype(ml_dtypes.bfloat16).astype(np.float64), axis, -1)
    blocks = v.reshape(v.shape[:-1] + (-1, 32))
    amax = np.abs(blocks).max(-1, keepdims=True)
    byte = np.maximum(np.where(amax > 0, np.frexp(amax)[1] - 1 + 127, 0) - down, 1)
    scale = np.exp2(byte - 127.0)
    codes = (blocks / scale).astype(np.float32).astype(dtype).astype(np.float64)
    return np.moveaxis((codes * scale).reshape(v.shape), -1, axis)


WIDE = False


def mx_kscale(k):
    if not WIDE:
        return np.ones(k)
    levels = np.array([20, -20, 10, -10, 0])
    a = np.random.permutation(np.resize(levels, k // 512 * 4)).reshape(k // 512, 4)
    idx = np.arange(k)
    return np.exp2(a[idx // 512, idx % 128 // 32])


BF16 = ml_dtypes.bfloat16


def bf(x):
    return np.asarray(x, np.float32).astype(BF16)


def f64(x):
    return np.asarray(x).astype(np.float64)


N, H, W, K = 512, 512, 8, 512
TAU = 1.0


def sigmoid(v):
    return 1.0 / (1.0 + np.exp(-v))


def silu(v):
    return v / (1.0 + np.exp(-v))


def softmax_last(v):
    e = np.exp(v - v.max(-1, keepdims=True))
    return e / e.sum(-1, keepdims=True)


def scores(xf, tf):
    xw = xf.reshape(xf.shape[0], W, K)
    tw = tf.reshape(tf.shape[0], W, K)
    return (xw.transpose(1, 0, 2) @ tw.transpose(1, 2, 0)).transpose(1, 2, 0)


def setup_inputs():
    f = mx_kscale(N)[:, None]
    x0 = bf(np.random.standard_normal((N, W * K)))
    t = bf(np.random.standard_normal((H, W * K)) / np.sqrt(K))
    g = bf(np.random.standard_normal((N, H)) * np.exp2(np.random.randint(-12, 1, (N, 1))) * 4.0 / f)
    s = scores(f64(x0), f64(t))
    return {"x": bf(f64(x0) * f), "template_flat": t, "s": np.asarray(s, np.float32), "grad_out": g}


def reference(x, template_flat, s, grad_out):
    sf = f64(s)
    gate = softmax_last(sf / TAU)
    sg = sigmoid(sf)
    act = sf * sg
    dact = sg * (1.0 + sf * (1.0 - sg))
    y = np.sum(gate * act, axis=-1, keepdims=True)
    ds = f64(grad_out)[:, :, None] * (gate * (dact + (act - y) / TAU))
    xw = f64(x).reshape(x.shape[0], W, K)
    dq = mxq(ds, 0, "e5m2")
    xq = mxq(xw, 0, "e4m3")
    dt = dq.transpose(2, 1, 0) @ xq.transpose(1, 0, 2)
    return dt.transpose(1, 0, 2).reshape(ds.shape[1], W * K)

@@ -1,0 +1,157 @@
+from contextlib import ExitStack
+
+import concourse.mybir as mybir
+
+F32 = mybir.dt.float32
+BF16 = mybir.dt.bfloat16
+U32 = mybir.dt.uint32
+U8 = mybir.dt.uint8
+E4M3_X4 = mybir.dt.float8_e4m3fn_x4
+E5M2_X4 = mybir.dt.float8_e5m2_x4
+ALU = mybir.AluOpType
+ACT = mybir.ActivationFunctionType
+AXIS = mybir.AxisListType
+
+P = 128
+PACK = 4
+TOKENS = P * PACK
+H = 512
+W = 8
+K = 512
+H_TILE = 128
+H_CHUNK = 64
+ROWS = PACK * H_CHUNK
+STORE = 2048
+
+FLOPS = 2 * TOKENS * H * W * K
+BYTES = TOKENS * W * K * 2 + TOKENS * H * W * 4 + TOKENS * H * 2 + H * W * K * 4
+
+
+def tile_dendriticlayersilu_ffn_v_kernel(tc, x, template_flat, s, grad_out, out):
+    nc = tc.nc
+    x_rows = x.rearrange("(p j) c -> p j c", j=PACK)
+    s_rows = s.rearrange("(p j) h w -> p j h w", j=PACK)
+    g_rows = grad_out.rearrange("(p j) h -> p j h", j=PACK)
+
+    with ExitStack() as stack:
+        keep = stack.enter_context(tc.tile_pool(name="keep", bufs=1))
+        x_raw_pool = stack.enter_context(tc.tile_pool(name="x_raw", bufs=W))
+        x_grouped_pool = stack.enter_context(tc.tile_pool(name="x_grouped", bufs=2))
+        s_pool = stack.enter_context(tc.tile_pool(name="s", bufs=3))
+        work = stack.enter_context(tc.tile_pool(name="work", bufs=2))
+        small = stack.enter_context(tc.tile_pool(name="small", bufs=2))
+        ds_pool = stack.enter_context(tc.tile_pool(name="ds", bufs=2))
+        out_pool = stack.enter_context(tc.tile_pool(name="out", bufs=3))
+        psum = stack.enter_context(tc.psum_pool(name="psum", bufs=8))
+
+        g_sb = keep.tile([P, PACK, H], BF16)
+        x_codes = keep.tile([P, W, K], U32, align_bytes=64)
+        x_scales = keep.tile([P, W, K], U8, align_bytes=64)
+
+        def load_s(chunk):
+            s_sb = s_pool.tile([P, PACK, H_CHUNK, W], F32, name="s_sb")
+            h0 = chunk * H_CHUNK
+            nc.sync.dma_start(out=s_sb[:], in_=s_rows[:, :, h0 : h0 + H_CHUNK, :])
+            return s_sb
+
+        first_s = load_s(0)
+        nc.sync.dma_start(out=g_sb[:], in_=g_rows)
+
+        for w in range(W):
+            x_raw = x_raw_pool.tile([P, PACK, K], BF16)
+            nc.sync.dma_start(out=x_raw[:], in_=x_rows[:, :, w * K : (w + 1) * K])
+            x_grouped = x_grouped_pool.tile([P, K, PACK], BF16, align_bytes=64)
+            nc.scalar.copy(out=x_grouped[:], in_=x_raw[:].rearrange("p j c -> p c j"))
+            nc.vector.quantize_mx(
+                out=x_codes[:, w, :].bitcast(E4M3_X4),
+                scales=x_scales[:, w, :],
+                in_=x_grouped[:].rearrange("p c j -> p (c j)"),
+            )
+
+        for h_tile in range(H // H_TILE):
+            ds_grouped = ds_pool.tile([P, W, H_TILE, PACK], BF16, align_bytes=64)
+            for half in range(H_TILE // H_CHUNK):
+                chunk = h_tile * (H_TILE // H_CHUNK) + half
+                s_sb = first_s if chunk == 0 else load_s(chunk)
+                s_v = s_sb[:].rearrange("p j h w -> p (j h) w")
+                wide = [P, ROWS, W]
+
+                top = small.tile([P, ROWS], F32)
+                nc.vector.tensor_reduce(out=top[:], in_=s_v, axis=AXIS.X, op=ALU.max)
+                e = work.tile([P, ROWS, W], F32)
+                nc.vector.tensor_tensor(
+                    out=e[:], in0=s_v, in1=top[:].unsqueeze(2).to_broadcast(wide), op=ALU.subtract
+                )
+                sg = work.tile([P, ROWS, W], F32)
+                nc.scalar.activation(out=sg[:], in_=s_v, func=ACT.Sigmoid)
+                act = work.tile([P, ROWS, W], F32)
+                nc.scalar.activation(out=act[:], in_=s_v, func=ACT.Silu)
+                nc.scalar.activation(out=e[:], in_=e[:], func=ACT.Exp)
+                z = small.tile([P, ROWS], F32)
+                nc.vector.tensor_reduce(out=z[:], in_=e[:], axis=AXIS.X, op=ALU.add)
+
+                t = work.tile([P, ROWS, W], F32)
+                nc.vector.scalar_tensor_tensor(
+                    out=t[:], in0=sg[:], scalar=-2.0, in1=act[:], op0=ALU.add, op1=ALU.mult
+                )
+                nc.vector.tensor_tensor(out=t[:], in0=t[:], in1=sg[:], op=ALU.subtract)
+
+                nc.vector.tensor_tensor(out=act[:], in0=act[:], in1=e[:], op=ALU.mult)
+                y = small.tile([P, ROWS], F32)
+                nc.vector.tensor_reduce(out=y[:], in_=act[:], axis=AXIS.X, op=ALU.add)
+                rz = small.tile([P, ROWS], F32)
+                nc.vector.reciprocal(out=rz[:], in_=z[:])
+                nc.vector.tensor_tensor(out=y[:], in0=y[:], in1=rz[:], op=ALU.mult)
+                c = small.tile([P, PACK, H_CHUNK], F32)
+                h0 = chunk * H_CHUNK
+                nc.vector.scalar_tensor_tensor(
+                    out=c[:],
+                    in0=g_sb[:, :, h0 : h0 + H_CHUNK],
+                    scalar=-1.0,
+                    in1=rz[:].rearrange("p (j h) -> p j h", j=PACK),
+                    op0=ALU.mult,
+                    op1=ALU.mult,
+                )
+
+                nc.vector.tensor_tensor(
+                    out=t[:], in0=t[:], in1=y[:].unsqueeze(2).to_broadcast(wide), op=ALU.add
+                )
+                nc.vector.tensor_tensor(out=t[:], in0=t[:], in1=e[:], op=ALU.mult)
+                t_v = t[:].rearrange("p (j h) w -> p h w j", j=PACK)
+                c_v = c[:].rearrange("p j h -> p h j").unsqueeze(2)
+                f0 = half * H_CHUNK
+                for w0 in range(0, W, 4):
+                    nc.vector.tensor_tensor(
+                        out=ds_grouped[:, w0 : w0 + 4, f0 : f0 + H_CHUNK, :].rearrange(
+                            "p w h j -> p h w j"
+                        ),
+                        in0=t_v[:, :, w0 : w0 + 4, :],
+                        in1=c_v.to_broadcast([P, H_CHUNK, 4, PACK]),
+                        op=ALU.mult,
+                    )
+
+            ds_codes = ds_pool.tile([P, W, H_TILE], U32, align_bytes=64)
+            ds_scales = ds_pool.tile([P, W, H_TILE], U8, align_bytes=64)
+            nc.vector.quantize_mx(
+                out=ds_codes[:].rearrange("p w h -> p (w h)").bitcast(E5M2_X4),
+                scales=ds_scales[:].rearrange("p w h -> p (w h)"),
+                in_=ds_grouped[:].rearrange("p w h j -> p (w h j)"),
+            )
+
+            rows = slice(h_tile * H_TILE, (h_tile + 1) * H_TILE)
+            for w0 in range(0, W, STORE // K):
+                out_sb = out_pool.tile([P, STORE], F32)
+                for i in range(STORE // K):
+                    w = w0 + i
+                    acc = psum.tile([H_TILE, K], F32)
+                    nc.tensor.matmul_mx(
+                        out=acc[:],
+                        lhsT=ds_codes[:, w, :].bitcast(E5M2_X4),
+                        lhsT_scale=ds_scales[:, w, :],
+                        rhs=x_codes[:, w, :].bitcast(E4M3_X4),
+                        rhs_scale=x_scales[:, w, :],
+                        start=True,
+                        stop=True,
+                    )
+                    nc.scalar.copy(out=out_sb[:, i * K : (i + 1) * K], in_=acc[:])
+                nc.scalar.dma_start(out=out[rows, w0 * K : w0 * K + STORE], in_=out_sb[:])

@@ -1,6 +1,7 @@
 from contextlib import ExitStack
 
 import concourse.mybir as mybir
+from concourse.masks import make_identity
 
 F32 = mybir.dt.float32
 BF16 = mybir.dt.bfloat16
@@ -20,7 +21,9 @@ W = 8
 K = 512
 H_TILE = 128
 H_CHUNK = 64
+CHUNKS = H // H_CHUNK
 ROWS = PACK * H_CHUNK
+BLOCKS = ROWS // P
 STORE = 2048
 
 FLOPS = 2 * TOKENS * H * W * K
@@ -32,29 +35,136 @@ def tile_dendriticlayersilu_ffn_v_kernel(tc, x, template_flat, s, grad_out, out)
     x_rows = x.rearrange("(p j) c -> p j c", j=PACK)
     s_rows = s.rearrange("(p j) h w -> p j h w", j=PACK)
     g_rows = grad_out.rearrange("(p j) h -> p j h", j=PACK)
+    wide = [P, ROWS, W]
 
     with ExitStack() as stack:
         keep = stack.enter_context(tc.tile_pool(name="keep", bufs=1))
         x_raw_pool = stack.enter_context(tc.tile_pool(name="x_raw", bufs=W))
         x_grouped_pool = stack.enter_context(tc.tile_pool(name="x_grouped", bufs=2))
         s_pool = stack.enter_context(tc.tile_pool(name="s", bufs=3))
-        work = stack.enter_context(tc.tile_pool(name="work", bufs=2))
+        long_pool = stack.enter_context(tc.tile_pool(name="long", bufs=3))
+        short_pool = stack.enter_context(tc.tile_pool(name="short", bufs=2))
         small = stack.enter_context(tc.tile_pool(name="small", bufs=2))
         ds_pool = stack.enter_context(tc.tile_pool(name="ds", bufs=2))
         out_pool = stack.enter_context(tc.tile_pool(name="out", bufs=3))
-        psum = stack.enter_context(tc.psum_pool(name="psum", bufs=8))
+        sums_psum = stack.enter_context(tc.psum_pool(name="sums_psum", bufs=2))
+        acc_psum = stack.enter_context(tc.psum_pool(name="acc_psum", bufs=4))
 
+        identity = keep.tile([P, P], F32)
+        make_identity(nc, identity[:])
         g_sb = keep.tile([P, PACK, H], BF16)
         x_codes = keep.tile([P, W, K], U32, align_bytes=64)
         x_scales = keep.tile([P, W, K], U8, align_bytes=64)
 
-        def load_s(chunk):
+        def first_half(chunk):
             s_sb = s_pool.tile([P, PACK, H_CHUNK, W], F32, name="s_sb")
             h0 = chunk * H_CHUNK
             nc.sync.dma_start(out=s_sb[:], in_=s_rows[:, :, h0 : h0 + H_CHUNK, :])
-            return s_sb
+            s_v = s_sb[:].rearrange("p j h w -> p (j h) w")
 
-        first_s = load_s(0)
+            top = small.tile([P, ROWS], F32, name="top")
+            nc.vector.tensor_reduce(out=top[:], in_=s_v, axis=AXIS.X, op=ALU.max)
+            e = long_pool.tile(wide, F32, name="e")
+            nc.vector.tensor_tensor(
+                out=e[:], in0=s_v, in1=top[:].unsqueeze(2).to_broadcast(wide), op=ALU.subtract
+            )
+            p2 = long_pool.tile(wide, F32, name="p2")
+            nc.scalar.activation(out=p2[:], in_=s_v, func=ACT.Tanh, scale=0.5)
+            act1 = short_pool.tile(wide, F32, name="act1")
+            nc.scalar.activation(out=act1[:], in_=s_v, func=ACT.Silu)
+            nc.scalar.add(out=act1[:], in_=act1[:], add=-1.0)
+            nc.scalar.activation(out=e[:], in_=e[:], func=ACT.Exp)
+
+            nc.vector.scalar_tensor_tensor(
+                out=p2[:], in0=p2[:], scalar=-3.0, in1=act1[:], op0=ALU.add, op1=ALU.mult
+            )
+            nc.vector.tensor_tensor(out=act1[:], in0=act1[:], in1=e[:], op=ALU.mult)
+
+            sums_t = sums_psum.tile([P, 2 * ROWS], F32, name="sums_t")
+            for i, terms in enumerate((e, act1)):
+                for b in range(BLOCKS):
+                    col = (i * BLOCKS + b) * P
+                    for w in range(W):
+                        nc.tensor.matmul(
+                            out=sums_t[:, col : col + P],
+                            lhsT=terms[:, b * P : (b + 1) * P, w],
+                            rhs=identity[:],
+                            is_transpose=True,
+                            start=(w == 0),
+                            stop=(w == W - 1),
+                        )
+            sums_t_sb = small.tile([P, 2 * ROWS], F32, name="sums_t_sb")
+            nc.scalar.copy(out=sums_t_sb[:], in_=sums_t[:])
+            sums = sums_psum.tile([P, 2 * ROWS], F32, name="sums")
+            for b in range(2 * BLOCKS):
+                cols = slice(b * P, (b + 1) * P)
+                nc.tensor.transpose(out=sums[:, cols], in_=sums_t_sb[:, cols], identity=identity[:])
+            return e, p2, sums
+
+        def second_half(chunk, e, p2, sums, ds_grouped):
+            rz = small.tile([P, ROWS], F32, name="rz")
+            nc.vector.reciprocal(out=rz[:], in_=sums[:, 0:ROWS])
+            y2 = small.tile([P, ROWS], F32, name="y2")
+            nc.vector.scalar_tensor_tensor(
+                out=y2[:], in0=sums[:, ROWS : 2 * ROWS], scalar=2.0, in1=rz[:], op0=ALU.mult, op1=ALU.mult
+            )
+            c = small.tile([P, PACK, H_CHUNK], F32, name="c")
+            h0 = chunk * H_CHUNK
+            nc.vector.scalar_tensor_tensor(
+                out=c[:],
+                in0=g_sb[:, :, h0 : h0 + H_CHUNK],
+                scalar=-0.5,
+                in1=rz[:].rearrange("p (j h) -> p j h", j=PACK),
+                op0=ALU.mult,
+                op1=ALU.mult,
+            )
+            nc.vector.scalar_tensor_tensor(
+                out=p2[:],
+                in0=p2[:],
+                scalar=-2.0,
+                in1=y2[:].unsqueeze(2).to_broadcast(wide),
+                op0=ALU.add,
+                op1=ALU.add,
+            )
+            nc.vector.tensor_tensor(out=p2[:], in0=p2[:], in1=e[:], op=ALU.mult)
+            t_v = p2[:].rearrange("p (j h) w -> p h w j", j=PACK)
+            c_v = c[:].rearrange("p j h -> p h j").unsqueeze(2)
+            f0 = (chunk * H_CHUNK) % H_TILE
+            for w0 in range(0, W, 4):
+                nc.vector.tensor_tensor(
+                    out=ds_grouped[:, w0 : w0 + 4, f0 : f0 + H_CHUNK, :].rearrange("p w h j -> p h w j"),
+                    in0=t_v[:, :, w0 : w0 + 4, :],
+                    in1=c_v.to_broadcast([P, H_CHUNK, 4, PACK]),
+                    op=ALU.mult,
+                )
+
+        def multiply(h_tile, ds_grouped):
+            ds_codes = ds_pool.tile([P, W, H_TILE], U32, align_bytes=64, name="ds_codes")
+            ds_scales = ds_pool.tile([P, W, H_TILE], U8, align_bytes=64, name="ds_scales")
+            nc.vector.quantize_mx(
+                out=ds_codes[:].rearrange("p w h -> p (w h)").bitcast(E5M2_X4),
+                scales=ds_scales[:].rearrange("p w h -> p (w h)"),
+                in_=ds_grouped[:].rearrange("p w h j -> p (w h j)"),
+            )
+            rows = slice(h_tile * H_TILE, (h_tile + 1) * H_TILE)
+            for w0 in range(0, W, STORE // K):
+                out_sb = out_pool.tile([P, STORE], F32, name="out_sb")
+                for i in range(STORE // K):
+                    w = w0 + i
+                    acc = acc_psum.tile([H_TILE, K], F32, name="acc")
+                    nc.tensor.matmul_mx(
+                        out=acc[:],
+                        lhsT=ds_codes[:, w, :].bitcast(E5M2_X4),
+                        lhsT_scale=ds_scales[:, w, :],
+                        rhs=x_codes[:, w, :].bitcast(E4M3_X4),
+                        rhs_scale=x_scales[:, w, :],
+                        start=True,
+                        stop=True,
+                    )
+                    nc.scalar.copy(out=out_sb[:, i * K : (i + 1) * K], in_=acc[:])
+                nc.scalar.dma_start(out=out[rows, w0 * K : w0 * K + STORE], in_=out_sb[:])
+
+        ahead = first_half(0)
         nc.sync.dma_start(out=g_sb[:], in_=g_rows)
 
         for w in range(W):
@@ -68,90 +178,13 @@ def tile_dendriticlayersilu_ffn_v_kernel(tc, x, template_flat, s, grad_out, out)
                 in_=x_grouped[:].rearrange("p c j -> p (c j)"),
             )
 
-        for h_tile in range(H // H_TILE):
-            ds_grouped = ds_pool.tile([P, W, H_TILE, PACK], BF16, align_bytes=64)
-            for half in range(H_TILE // H_CHUNK):
-                chunk = h_tile * (H_TILE // H_CHUNK) + half
-                s_sb = first_s if chunk == 0 else load_s(chunk)
-                s_v = s_sb[:].rearrange("p j h w -> p (j h) w")
-                wide = [P, ROWS, W]
-
-                top = small.tile([P, ROWS], F32)
-                nc.vector.tensor_reduce(out=top[:], in_=s_v, axis=AXIS.X, op=ALU.max)
-                e = work.tile([P, ROWS, W], F32)
-                nc.vector.tensor_tensor(
-                    out=e[:], in0=s_v, in1=top[:].unsqueeze(2).to_broadcast(wide), op=ALU.subtract
-                )
-                sg = work.tile([P, ROWS, W], F32)
-                nc.scalar.activation(out=sg[:], in_=s_v, func=ACT.Sigmoid)
-                act = work.tile([P, ROWS, W], F32)
-                nc.scalar.activation(out=act[:], in_=s_v, func=ACT.Silu)
-                nc.scalar.activation(out=e[:], in_=e[:], func=ACT.Exp)
-                z = small.tile([P, ROWS], F32)
-                nc.vector.tensor_reduce(out=z[:], in_=e[:], axis=AXIS.X, op=ALU.add)
-
-                t = work.tile([P, ROWS, W], F32)
-                nc.vector.scalar_tensor_tensor(
-                    out=t[:], in0=sg[:], scalar=-2.0, in1=act[:], op0=ALU.add, op1=ALU.mult
-                )
-                nc.vector.tensor_tensor(out=t[:], in0=t[:], in1=sg[:], op=ALU.subtract)
-
-                nc.vector.tensor_tensor(out=act[:], in0=act[:], in1=e[:], op=ALU.mult)
-                y = small.tile([P, ROWS], F32)
-                nc.vector.tensor_reduce(out=y[:], in_=act[:], axis=AXIS.X, op=ALU.add)
-                rz = small.tile([P, ROWS], F32)
-                nc.vector.reciprocal(out=rz[:], in_=z[:])
-                nc.vector.tensor_tensor(out=y[:], in0=y[:], in1=rz[:], op=ALU.mult)
-                c = small.tile([P, PACK, H_CHUNK], F32)
-                h0 = chunk * H_CHUNK
-                nc.vector.scalar_tensor_tensor(
-                    out=c[:],
-                    in0=g_sb[:, :, h0 : h0 + H_CHUNK],
-                    scalar=-1.0,
-                    in1=rz[:].rearrange("p (j h) -> p j h", j=PACK),
-                    op0=ALU.mult,
-                    op1=ALU.mult,
-                )
-
-                nc.vector.tensor_tensor(
-                    out=t[:], in0=t[:], in1=y[:].unsqueeze(2).to_broadcast(wide), op=ALU.add
-                )
-                nc.vector.tensor_tensor(out=t[:], in0=t[:], in1=e[:], op=ALU.mult)
-                t_v = t[:].rearrange("p (j h) w -> p h w j", j=PACK)
-                c_v = c[:].rearrange("p j h -> p h j").unsqueeze(2)
-                f0 = half * H_CHUNK
-                for w0 in range(0, W, 4):
-                    nc.vector.tensor_tensor(
-                        out=ds_grouped[:, w0 : w0 + 4, f0 : f0 + H_CHUNK, :].rearrange(
-                            "p w h j -> p h w j"
-                        ),
-                        in0=t_v[:, :, w0 : w0 + 4, :],
-                        in1=c_v.to_broadcast([P, H_CHUNK, 4, PACK]),
-                        op=ALU.mult,
-                    )
-
-            ds_codes = ds_pool.tile([P, W, H_TILE], U32, align_bytes=64)
-            ds_scales = ds_pool.tile([P, W, H_TILE], U8, align_bytes=64)
-            nc.vector.quantize_mx(
-                out=ds_codes[:].rearrange("p w h -> p (w h)").bitcast(E5M2_X4),
-                scales=ds_scales[:].rearrange("p w h -> p (w h)"),
-                in_=ds_grouped[:].rearrange("p w h j -> p (w h j)"),
-            )
-
-            rows = slice(h_tile * H_TILE, (h_tile + 1) * H_TILE)
-            for w0 in range(0, W, STORE // K):
-                out_sb = out_pool.tile([P, STORE], F32)
-                for i in range(STORE // K):
-                    w = w0 + i
-                    acc = psum.tile([H_TILE, K], F32)
-                    nc.tensor.matmul_mx(
-                        out=acc[:],
-                        lhsT=ds_codes[:, w, :].bitcast(E5M2_X4),
-                        lhsT_scale=ds_scales[:, w, :],
-                        rhs=x_codes[:, w, :].bitcast(E4M3_X4),
-                        rhs_scale=x_scales[:, w, :],
-                        start=True,
-                        stop=True,
-                    )
-                    nc.scalar.copy(out=out_sb[:, i * K : (i + 1) * K], in_=acc[:])
-                nc.scalar.dma_start(out=out[rows, w0 * K : w0 * K + STORE], in_=out_sb[:])
+        ds_grouped = None
+        for chunk in range(CHUNKS):
+            e, p2, sums = ahead
+            if chunk + 1 < CHUNKS:
+                ahead = first_half(chunk + 1)
+            if (chunk * H_CHUNK) % H_TILE == 0:
+                ds_grouped = ds_pool.tile([P, W, H_TILE, PACK], BF16, align_bytes=64, name="ds_grouped")
+            second_half(chunk, e, p2, sums, ds_grouped)
+            if ((chunk + 1) * H_CHUNK) % H_TILE == 0:
+                multiply((chunk * H_CHUNK) // H_TILE, ds_grouped)

@@ -22,9 +22,12 @@ K = 512
 H_TILE = 128
 H_CHUNK = 64
 CHUNKS = H // H_CHUNK
+CHUNKS_PER_TILE = H_TILE // H_CHUNK
 ROWS = PACK * H_CHUNK
 BLOCKS = ROWS // P
-STORE = 2048
+ACC_BANKS = 4
+STORE_BANKS = 2
+X_PER_ROUND = 3
 
 FLOPS = 2 * TOKENS * H * W * K
 BYTES = TOKENS * W * K * 2 + TOKENS * H * W * 4 + TOKENS * H * 2 + H * W * K * 4
@@ -38,17 +41,14 @@ def tile_dendriticlayersilu_ffn_v_kernel(tc, x, template_flat, s, grad_out, out)
     wide = [P, ROWS, W]
 
     with ExitStack() as stack:
+        stack.enter_context(tc.manual_schedule())
         keep = stack.enter_context(tc.tile_pool(name="keep", bufs=1))
         x_raw_pool = stack.enter_context(tc.tile_pool(name="x_raw", bufs=W))
-        x_grouped_pool = stack.enter_context(tc.tile_pool(name="x_grouped", bufs=2))
-        s_pool = stack.enter_context(tc.tile_pool(name="s", bufs=3))
-        long_pool = stack.enter_context(tc.tile_pool(name="long", bufs=3))
-        short_pool = stack.enter_context(tc.tile_pool(name="short", bufs=2))
-        small = stack.enter_context(tc.tile_pool(name="small", bufs=2))
-        ds_pool = stack.enter_context(tc.tile_pool(name="ds", bufs=2))
-        out_pool = stack.enter_context(tc.tile_pool(name="out", bufs=3))
+        four = stack.enter_context(tc.tile_pool(name="four", bufs=4))
+        three = stack.enter_context(tc.tile_pool(name="three", bufs=3))
+        two = stack.enter_context(tc.tile_pool(name="two", bufs=2))
         sums_psum = stack.enter_context(tc.psum_pool(name="sums_psum", bufs=2))
-        acc_psum = stack.enter_context(tc.psum_pool(name="acc_psum", bufs=4))
+        acc_psum = stack.enter_context(tc.psum_pool(name="acc_psum", bufs=ACC_BANKS))
 
         identity = keep.tile([P, P], F32)
         make_identity(nc, identity[:])
@@ -56,135 +56,235 @@ def tile_dendriticlayersilu_ffn_v_kernel(tc, x, template_flat, s, grad_out, out)
         x_codes = keep.tile([P, W, K], U32, align_bytes=64)
         x_scales = keep.tile([P, W, K], U8, align_bytes=64)
 
-        def first_half(chunk):
-            s_sb = s_pool.tile([P, PACK, H_CHUNK, W], F32, name="s_sb")
-            h0 = chunk * H_CHUNK
-            nc.sync.dma_start(out=s_sb[:], in_=s_rows[:, :, h0 : h0 + H_CHUNK, :])
-            s_v = s_sb[:].rearrange("p j h w -> p (j h) w")
+        s_sb, top, e, m1, a1 = {}, {}, {}, {}, {}
+        sums_t, sums, guess, nrz, y2, c = {}, {}, {}, {}, {}, {}
+        x_raw, x_grouped, ds_grouped = {}, {}, {}
 
-            top = small.tile([P, ROWS], F32, name="top")
-            nc.vector.tensor_reduce(out=top[:], in_=s_v, axis=AXIS.X, op=ALU.max)
-            e = long_pool.tile(wide, F32, name="e")
-            nc.vector.tensor_tensor(
-                out=e[:], in0=s_v, in1=top[:].unsqueeze(2).to_broadcast(wide), op=ALU.subtract
+        def spread(small):
+            return small[:].unsqueeze(2).to_broadcast(wide)
+
+        def load_s(k):
+            s_sb[k] = three.tile([P, ROWS, W], F32, name="s_sb")
+            nc.sync.dma_start(
+                out=s_sb[k][:].rearrange("p (j h) w -> p j h w", j=PACK),
+                in_=s_rows[:, :, k * H_CHUNK : (k + 1) * H_CHUNK, :],
             )
-            p2 = long_pool.tile(wide, F32, name="p2")
-            nc.scalar.activation(out=p2[:], in_=s_v, func=ACT.Tanh, scale=0.5)
-            act1 = short_pool.tile(wide, F32, name="act1")
-            nc.scalar.activation(out=act1[:], in_=s_v, func=ACT.Silu)
-            nc.scalar.add(out=act1[:], in_=act1[:], add=-1.0)
-            nc.scalar.activation(out=e[:], in_=e[:], func=ACT.Exp)
 
-            nc.vector.scalar_tensor_tensor(
-                out=p2[:], in0=p2[:], scalar=-3.0, in1=act1[:], op0=ALU.add, op1=ALU.mult
-            )
-            nc.vector.tensor_tensor(out=act1[:], in0=act1[:], in1=e[:], op=ALU.mult)
+        def load_x(w):
+            x_raw[w] = x_raw_pool.tile([P, PACK, K], BF16, name="x_raw")
+            nc.sync.dma_start(out=x_raw[w][:], in_=x_rows[:, :, w * K : (w + 1) * K])
 
-            sums_t = sums_psum.tile([P, 2 * ROWS], F32, name="sums_t")
-            for i, terms in enumerate((e, act1)):
+        def tanh_and_silu(k):
+            m1[k] = four.tile(wide, F32, name="m1")
+            nc.scalar.activation(out=m1[k][:], in_=s_sb[k][:], func=ACT.Tanh, scale=0.5)
+            a1[k] = two.tile(wide, F32, name="a1")
+            nc.scalar.activation(out=a1[k][:], in_=s_sb[k][:], func=ACT.Silu)
+
+        def exponential(k):
+            nc.scalar.activation(out=e[k][:], in_=e[k][:], func=ACT.Exp)
+
+        def guess_reciprocal(k):
+            guess[k] = two.tile([P, ROWS], F32, name="guess")
+            nc.scalar.activation(out=guess[k][:], in_=sums[k][:, 0:ROWS], func=ACT.Ln)
+            nc.scalar.activation(out=guess[k][:], in_=guess[k][:], func=ACT.Exp, scale=-1.0)
+
+        def add_windows(k):
+            sums_t[k] = sums_psum.tile([P, 2 * ROWS], F32, name="sums_t")
+            for i, terms in enumerate((e[k], a1[k])):
                 for b in range(BLOCKS):
                     col = (i * BLOCKS + b) * P
                     for w in range(W):
                         nc.tensor.matmul(
-                            out=sums_t[:, col : col + P],
+                            out=sums_t[k][:, col : col + P],
                             lhsT=terms[:, b * P : (b + 1) * P, w],
                             rhs=identity[:],
                             is_transpose=True,
                             start=(w == 0),
                             stop=(w == W - 1),
                         )
-            sums_t_sb = small.tile([P, 2 * ROWS], F32, name="sums_t_sb")
-            nc.scalar.copy(out=sums_t_sb[:], in_=sums_t[:])
-            sums = sums_psum.tile([P, 2 * ROWS], F32, name="sums")
+
+        def turn_sums_back(k):
+            sums_t_sb = two.tile([P, 2 * ROWS], F32, name="sums_t_sb")
+            nc.scalar.copy(out=sums_t_sb[:], in_=sums_t[k][:])
+            sums[k] = sums_psum.tile([P, 2 * ROWS], F32, name="sums")
             for b in range(2 * BLOCKS):
                 cols = slice(b * P, (b + 1) * P)
-                nc.tensor.transpose(out=sums[:, cols], in_=sums_t_sb[:, cols], identity=identity[:])
-            return e, p2, sums
+                nc.tensor.transpose(out=sums[k][:, cols], in_=sums_t_sb[:, cols], identity=identity[:])
 
-        def second_half(chunk, e, p2, sums, ds_grouped):
-            rz = small.tile([P, ROWS], F32, name="rz")
-            nc.vector.reciprocal(out=rz[:], in_=sums[:, 0:ROWS])
-            y2 = small.tile([P, ROWS], F32, name="y2")
+        def maximum(k):
+            top[k] = two.tile([P, ROWS], F32, name="top")
+            nc.vector.tensor_reduce(out=top[k][:], in_=s_sb[k][:], axis=AXIS.X, op=ALU.max)
+
+        def shift(k):
+            e[k] = four.tile(wide, F32, name="e")
+            nc.vector.tensor_tensor(out=e[k][:], in0=s_sb[k][:], in1=spread(top[k]), op=ALU.subtract)
+
+        def weigh_silu(k):
             nc.vector.scalar_tensor_tensor(
-                out=y2[:], in0=sums[:, ROWS : 2 * ROWS], scalar=2.0, in1=rz[:], op0=ALU.mult, op1=ALU.mult
+                out=a1[k][:], in0=a1[k][:], scalar=-1.0, in1=e[k][:], op0=ALU.add, op1=ALU.mult
             )
-            c = small.tile([P, PACK, H_CHUNK], F32, name="c")
-            h0 = chunk * H_CHUNK
+
+        def weigh_tanh(k):
             nc.vector.scalar_tensor_tensor(
-                out=c[:],
-                in0=g_sb[:, :, h0 : h0 + H_CHUNK],
-                scalar=-0.5,
-                in1=rz[:].rearrange("p (j h) -> p j h", j=PACK),
+                out=m1[k][:], in0=m1[k][:], scalar=-3.0, in1=a1[k][:], op0=ALU.add, op1=ALU.mult
+            )
+
+        def newton_product(k):
+            nrz[k] = two.tile([P, ROWS], F32, name="nrz")
+            nc.vector.tensor_tensor(out=nrz[k][:], in0=sums[k][:, 0:ROWS], in1=guess[k][:], op=ALU.mult)
+
+        def newton_step(k):
+            nc.vector.scalar_tensor_tensor(
+                out=nrz[k][:], in0=nrz[k][:], scalar=-2.0, in1=guess[k][:], op0=ALU.add, op1=ALU.mult
+            )
+
+        def mean_and_factor(k):
+            y2[k] = two.tile([P, ROWS], F32, name="y2")
+            nc.vector.scalar_tensor_tensor(
+                out=y2[k][:], in0=sums[k][:, ROWS : 2 * ROWS], scalar=-2.0, in1=nrz[k][:], op0=ALU.mult, op1=ALU.mult
+            )
+            c[k] = two.tile([P, PACK, H_CHUNK], F32, name="c")
+            nc.vector.scalar_tensor_tensor(
+                out=c[k][:],
+                in0=g_sb[:, :, k * H_CHUNK : (k + 1) * H_CHUNK],
+                scalar=0.5,
+                in1=nrz[k][:].rearrange("p (j h) -> p j h", j=PACK),
                 op0=ALU.mult,
                 op1=ALU.mult,
             )
+
+        def weigh_mean(k):
             nc.vector.scalar_tensor_tensor(
-                out=p2[:],
-                in0=p2[:],
-                scalar=-2.0,
-                in1=y2[:].unsqueeze(2).to_broadcast(wide),
-                op0=ALU.add,
-                op1=ALU.add,
+                out=e[k][:], in0=spread(y2[k]), scalar=-2.0, in1=e[k][:], op0=ALU.add, op1=ALU.mult
             )
-            nc.vector.tensor_tensor(out=p2[:], in0=p2[:], in1=e[:], op=ALU.mult)
-            t_v = p2[:].rearrange("p (j h) w -> p h w j", j=PACK)
-            c_v = c[:].rearrange("p j h -> p h j").unsqueeze(2)
-            f0 = (chunk * H_CHUNK) % H_TILE
+
+        def join(k):
+            nc.vector.tensor_tensor(out=m1[k][:], in0=m1[k][:], in1=e[k][:], op=ALU.add)
+
+        def write_ds(k):
+            tile_no = k // CHUNKS_PER_TILE
+            if k % CHUNKS_PER_TILE == 0:
+                ds_grouped[tile_no] = two.tile([P, W, H_TILE, PACK], BF16, align_bytes=64, name="ds_grouped")
+            f0 = (k % CHUNKS_PER_TILE) * H_CHUNK
+            m1_v = m1[k][:].rearrange("p (j h) w -> p h w j", j=PACK)
+            c_v = c[k][:].rearrange("p j h -> p h j").unsqueeze(2).to_broadcast([P, H_CHUNK, 4, PACK])
             for w0 in range(0, W, 4):
                 nc.vector.tensor_tensor(
-                    out=ds_grouped[:, w0 : w0 + 4, f0 : f0 + H_CHUNK, :].rearrange("p w h j -> p h w j"),
-                    in0=t_v[:, :, w0 : w0 + 4, :],
-                    in1=c_v.to_broadcast([P, H_CHUNK, 4, PACK]),
+                    out=ds_grouped[tile_no][:, w0 : w0 + 4, f0 : f0 + H_CHUNK, :].rearrange("p w h j -> p h w j"),
+                    in0=m1_v[:, :, w0 : w0 + 4, :],
+                    in1=c_v,
                     op=ALU.mult,
                 )
 
-        def multiply(h_tile, ds_grouped):
-            ds_codes = ds_pool.tile([P, W, H_TILE], U32, align_bytes=64, name="ds_codes")
-            ds_scales = ds_pool.tile([P, W, H_TILE], U8, align_bytes=64, name="ds_scales")
+        def quantise_ds(tile_no):
+            ds_codes = two.tile([P, W, H_TILE], U32, align_bytes=64, name="ds_codes")
+            ds_scales = two.tile([P, W, H_TILE], U8, align_bytes=64, name="ds_scales")
             nc.vector.quantize_mx(
                 out=ds_codes[:].rearrange("p w h -> p (w h)").bitcast(E5M2_X4),
                 scales=ds_scales[:].rearrange("p w h -> p (w h)"),
-                in_=ds_grouped[:].rearrange("p w h j -> p (w h j)"),
+                in_=ds_grouped[tile_no][:].rearrange("p w h j -> p (w h j)"),
             )
-            rows = slice(h_tile * H_TILE, (h_tile + 1) * H_TILE)
-            for w0 in range(0, W, STORE // K):
-                out_sb = out_pool.tile([P, STORE], F32, name="out_sb")
-                for i in range(STORE // K):
-                    w = w0 + i
-                    acc = acc_psum.tile([H_TILE, K], F32, name="acc")
-                    nc.tensor.matmul_mx(
-                        out=acc[:],
-                        lhsT=ds_codes[:, w, :].bitcast(E5M2_X4),
-                        lhsT_scale=ds_scales[:, w, :],
-                        rhs=x_codes[:, w, :].bitcast(E4M3_X4),
-                        rhs_scale=x_scales[:, w, :],
-                        start=True,
-                        stop=True,
-                    )
-                    nc.scalar.copy(out=out_sb[:, i * K : (i + 1) * K], in_=acc[:])
-                nc.scalar.dma_start(out=out[rows, w0 * K : w0 * K + STORE], in_=out_sb[:])
+            return ds_codes, ds_scales
 
-        ahead = first_half(0)
-        nc.sync.dma_start(out=g_sb[:], in_=g_rows)
+        def regroup_x(w):
+            x_grouped[w] = two.tile([P, K, PACK], BF16, align_bytes=64, name="x_grouped")
+            nc.vector.tensor_copy(
+                out=x_grouped[w][:].rearrange("p (c i) j -> p c j i", i=4),
+                in_=x_raw[w][:].rearrange("p j (c i) -> p c j i", i=4),
+            )
 
-        for w in range(W):
-            x_raw = x_raw_pool.tile([P, PACK, K], BF16)
-            nc.sync.dma_start(out=x_raw[:], in_=x_rows[:, :, w * K : (w + 1) * K])
-            x_grouped = x_grouped_pool.tile([P, K, PACK], BF16, align_bytes=64)
-            nc.scalar.copy(out=x_grouped[:], in_=x_raw[:].rearrange("p j c -> p c j"))
+        def quantise_x(w):
             nc.vector.quantize_mx(
                 out=x_codes[:, w, :].bitcast(E4M3_X4),
                 scales=x_scales[:, w, :],
-                in_=x_grouped[:].rearrange("p c j -> p (c j)"),
+                in_=x_grouped[w][:].rearrange("p c j -> p (c j)"),
             )
 
-        ds_grouped = None
-        for chunk in range(CHUNKS):
-            e, p2, sums = ahead
-            if chunk + 1 < CHUNKS:
-                ahead = first_half(chunk + 1)
-            if (chunk * H_CHUNK) % H_TILE == 0:
-                ds_grouped = ds_pool.tile([P, W, H_TILE, PACK], BF16, align_bytes=64, name="ds_grouped")
-            second_half(chunk, e, p2, sums, ds_grouped)
-            if ((chunk + 1) * H_CHUNK) % H_TILE == 0:
-                multiply((chunk * H_CHUNK) // H_TILE, ds_grouped)
+        def multiply_and_store(tile_no, ds_codes, ds_scales, copiers):
+            rows = slice(tile_no * H_TILE, (tile_no + 1) * H_TILE)
+            accs = []
+
+            def product(w):
+                acc = acc_psum.tile([H_TILE, K], F32, name="acc")
+                nc.tensor.matmul_mx(
+                    out=acc[:],
+                    lhsT=ds_codes[:, w, :].bitcast(E5M2_X4),
+                    lhsT_scale=ds_scales[:, w, :],
+                    rhs=x_codes[:, w, :].bitcast(E4M3_X4),
+                    rhs_scale=x_scales[:, w, :],
+                    start=True,
+                    stop=True,
+                )
+                accs.append(acc)
+
+            for w in range(ACC_BANKS):
+                product(w)
+            for w in range(W):
+                i = w % STORE_BANKS
+                if i == 0:
+                    out_sb = three.tile([P, STORE_BANKS * K], F32, name="out_sb")
+                copiers[w % len(copiers)](out=out_sb[:, i * K : (i + 1) * K], in_=accs[w][:])
+                if w + ACC_BANKS < W:
+                    product(w + ACC_BANKS)
+                if i == STORE_BANKS - 1:
+                    first = (w - i) * K
+                    nc.scalar.dma_start(out=out[rows, first : first + STORE_BANKS * K], in_=out_sb[:])
+
+        for r in range(CHUNKS + 3):
+            new = r if r < CHUNKS else None
+            mid = r - 1 if 0 <= r - 1 < CHUNKS else None
+            turn = r - 2 if 0 <= r - 2 < CHUNKS else None
+            old = r - 3 if r - 3 >= 0 else None
+            full = None
+            if old is not None and old > 0 and old % CHUNKS_PER_TILE == 0:
+                full = old // CHUNKS_PER_TILE - 1
+            windows = list(range(r * X_PER_ROUND, min((r + 1) * X_PER_ROUND, W)))
+
+            if turn is not None:
+                turn_sums_back(turn)
+            if new is not None:
+                load_s(new)
+                if new == 0:
+                    nc.sync.dma_start(out=g_sb[:], in_=g_rows)
+                tanh_and_silu(new)
+            for w in windows:
+                load_x(w)
+
+            if old is not None:
+                newton_product(old)
+            if new is not None:
+                maximum(new)
+            if old is not None:
+                newton_step(old)
+            if mid is not None:
+                weigh_silu(mid)
+                add_windows(mid)
+            if full is not None:
+                ds_codes, ds_scales = quantise_ds(full)
+            if old is not None:
+                mean_and_factor(old)
+                weigh_mean(old)
+            if new is not None:
+                shift(new)
+            if old is not None:
+                join(old)
+            if mid is not None:
+                weigh_tanh(mid)
+            if old is not None:
+                write_ds(old)
+            for w in windows:
+                regroup_x(w)
+                if w - 1 in windows:
+                    quantise_x(w - 1)
+            if windows:
+                quantise_x(windows[-1])
+
+            if turn is not None:
+                guess_reciprocal(turn)
+            if new is not None:
+                exponential(new)
+            if full is not None:
+                multiply_and_store(full, ds_codes, ds_scales, [nc.scalar.copy])
+
+        ds_codes, ds_scales = quantise_ds(H // H_TILE - 1)
+        multiply_and_store(H // H_TILE - 1, ds_codes, ds_scales, [nc.scalar.copy, nc.vector.tensor_copy])

@@ -43,8 +43,9 @@ def tile_dendriticlayersilu_ffn_v_kernel(tc, x, template_flat, s, grad_out, out)
     with ExitStack() as stack:
         stack.enter_context(tc.manual_schedule())
         keep = stack.enter_context(tc.tile_pool(name="keep", bufs=1))
-        x_raw_pool = stack.enter_context(tc.tile_pool(name="x_raw", bufs=W))
-        four = stack.enter_context(tc.tile_pool(name="four", bufs=4))
+        x_raw_pool = stack.enter_context(tc.tile_pool(name="x_raw", bufs=X_PER_ROUND))
+        six = stack.enter_context(tc.tile_pool(name="six", bufs=6))
+        five = stack.enter_context(tc.tile_pool(name="five", bufs=5))
         three = stack.enter_context(tc.tile_pool(name="three", bufs=3))
         two = stack.enter_context(tc.tile_pool(name="two", bufs=2))
         sums_psum = stack.enter_context(tc.psum_pool(name="sums_psum", bufs=2))
@@ -52,16 +53,19 @@ def tile_dendriticlayersilu_ffn_v_kernel(tc, x, template_flat, s, grad_out, out)
 
         identity = keep.tile([P, P], F32)
         make_identity(nc, identity[:])
-        g_sb = keep.tile([P, PACK, H], BF16)
+        identity_bf = keep.tile([P, P], BF16)
+        make_identity(nc, identity_bf[:])
+        g_sb = keep.tile([P, CHUNKS, PACK, H_CHUNK], BF16)
+        g_t = keep.tile([P, CHUNKS * BLOCKS, P], BF16)
         x_codes = keep.tile([P, W, K], U32, align_bytes=64)
         x_scales = keep.tile([P, W, K], U8, align_bytes=64)
 
         s_sb, top, e, m1, a1 = {}, {}, {}, {}, {}
-        sums_t, sums, guess, nrz, y2, c = {}, {}, {}, {}, {}, {}
+        sums_t, back, guess, nrz, yc_t = {}, {}, {}, {}, {}
         x_raw, x_grouped, ds_grouped = {}, {}, {}
 
         def spread(small):
-            return small[:].unsqueeze(2).to_broadcast(wide)
+            return small.unsqueeze(2).to_broadcast(wide)
 
         def load_s(k):
             s_sb[k] = three.tile([P, ROWS, W], F32, name="s_sb")
@@ -75,7 +79,7 @@ def tile_dendriticlayersilu_ffn_v_kernel(tc, x, template_flat, s, grad_out, out)
             nc.sync.dma_start(out=x_raw[w][:], in_=x_rows[:, :, w * K : (w + 1) * K])
 
         def tanh_and_silu(k):
-            m1[k] = four.tile(wide, F32, name="m1")
+            m1[k] = six.tile(wide, F32, name="m1")
             nc.scalar.activation(out=m1[k][:], in_=s_sb[k][:], func=ACT.Tanh, scale=0.5)
             a1[k] = two.tile(wide, F32, name="a1")
             nc.scalar.activation(out=a1[k][:], in_=s_sb[k][:], func=ACT.Silu)
@@ -85,7 +89,7 @@ def tile_dendriticlayersilu_ffn_v_kernel(tc, x, template_flat, s, grad_out, out)
 
         def guess_reciprocal(k):
             guess[k] = two.tile([P, ROWS], F32, name="guess")
-            nc.scalar.activation(out=guess[k][:], in_=sums[k][:, 0:ROWS], func=ACT.Ln)
+            nc.scalar.activation(out=guess[k][:], in_=sums_t[k][:, 0:ROWS], func=ACT.Ln)
             nc.scalar.activation(out=guess[k][:], in_=guess[k][:], func=ACT.Exp, scale=-1.0)
 
         def add_windows(k):
@@ -103,21 +107,29 @@ def tile_dendriticlayersilu_ffn_v_kernel(tc, x, template_flat, s, grad_out, out)
                             stop=(w == W - 1),
                         )
 
-        def turn_sums_back(k):
-            sums_t_sb = two.tile([P, 2 * ROWS], F32, name="sums_t_sb")
-            nc.scalar.copy(out=sums_t_sb[:], in_=sums_t[k][:])
-            sums[k] = sums_psum.tile([P, 2 * ROWS], F32, name="sums")
+        def turn_back(k):
+            back[k] = sums_psum.tile([P, 2 * ROWS], F32, name="back")
             for b in range(2 * BLOCKS):
                 cols = slice(b * P, (b + 1) * P)
-                nc.tensor.transpose(out=sums[k][:, cols], in_=sums_t_sb[:, cols], identity=identity[:])
+                nc.tensor.transpose(out=back[k][:, cols], in_=yc_t[k][:, cols], identity=identity[:])
+
+        def turn_grad_out():
+            for half in range(2):
+                g_ps = sums_psum.tile([P, CHUNKS * BLOCKS // 2, P], BF16, name="sums_t")
+                for i in range(CHUNKS * BLOCKS // 2):
+                    k, b = divmod(half * (CHUNKS * BLOCKS // 2) + i, BLOCKS)
+                    rows = g_sb[:, k, :, :].rearrange("p j h -> p (j h)")
+                    nc.tensor.transpose(out=g_ps[:, i, :], in_=rows[:, b * P : (b + 1) * P], identity=identity_bf[:])
+                n = CHUNKS * BLOCKS // 2
+                nc.scalar.copy(out=g_t[:, half * n : (half + 1) * n, :], in_=g_ps[:])
 
         def maximum(k):
             top[k] = two.tile([P, ROWS], F32, name="top")
             nc.vector.tensor_reduce(out=top[k][:], in_=s_sb[k][:], axis=AXIS.X, op=ALU.max)
 
         def shift(k):
-            e[k] = four.tile(wide, F32, name="e")
-            nc.vector.tensor_tensor(out=e[k][:], in0=s_sb[k][:], in1=spread(top[k]), op=ALU.subtract)
+            e[k] = five.tile(wide, F32, name="e")
+            nc.vector.tensor_tensor(out=e[k][:], in0=s_sb[k][:], in1=spread(top[k][:]), op=ALU.subtract)
 
         def weigh_silu(k):
             nc.vector.scalar_tensor_tensor(
@@ -131,35 +143,38 @@ def tile_dendriticlayersilu_ffn_v_kernel(tc, x, template_flat, s, grad_out, out)
 
         def newton_product(k):
             nrz[k] = two.tile([P, ROWS], F32, name="nrz")
-            nc.vector.tensor_tensor(out=nrz[k][:], in0=sums[k][:, 0:ROWS], in1=guess[k][:], op=ALU.mult)
+            nc.vector.tensor_tensor(out=nrz[k][:], in0=sums_t[k][:, 0:ROWS], in1=guess[k][:], op=ALU.mult)
 
         def newton_step(k):
             nc.vector.scalar_tensor_tensor(
                 out=nrz[k][:], in0=nrz[k][:], scalar=-2.0, in1=guess[k][:], op0=ALU.add, op1=ALU.mult
             )
 
-        def mean_and_factor(k):
-            y2[k] = two.tile([P, ROWS], F32, name="y2")
+        def mean(k):
+            yc_t[k] = two.tile([P, 2 * ROWS], F32, name="yc_t")
             nc.vector.scalar_tensor_tensor(
-                out=y2[k][:], in0=sums[k][:, ROWS : 2 * ROWS], scalar=-2.0, in1=nrz[k][:], op0=ALU.mult, op1=ALU.mult
-            )
-            c[k] = two.tile([P, PACK, H_CHUNK], F32, name="c")
-            nc.vector.scalar_tensor_tensor(
-                out=c[k][:],
-                in0=g_sb[:, :, k * H_CHUNK : (k + 1) * H_CHUNK],
-                scalar=0.5,
-                in1=nrz[k][:].rearrange("p (j h) -> p j h", j=PACK),
-                op0=ALU.mult,
-                op1=ALU.mult,
+                out=yc_t[k][:, ROWS : 2 * ROWS], in0=sums_t[k][:, ROWS : 2 * ROWS], scalar=-2.0, in1=nrz[k][:],
+                op0=ALU.mult, op1=ALU.mult,
             )
 
-        def weigh_mean(k):
+        def factor(k):
             nc.vector.scalar_tensor_tensor(
-                out=e[k][:], in0=spread(y2[k]), scalar=-2.0, in1=e[k][:], op0=ALU.add, op1=ALU.mult
+                out=yc_t[k][:, 0:ROWS],
+                in0=g_t[:, k * BLOCKS : (k + 1) * BLOCKS, :].rearrange("p b q -> p (b q)"),
+                scalar=0.5, in1=nrz[k][:], op0=ALU.mult, op1=ALU.mult,
             )
 
-        def join(k):
-            nc.vector.tensor_tensor(out=m1[k][:], in0=m1[k][:], in1=e[k][:], op=ALU.add)
+        def weigh_mean(k, half):
+            rows = slice(half * ROWS // 2, (half + 1) * ROWS // 2)
+            y2 = back[k][:, ROWS : 2 * ROWS]
+            nc.vector.scalar_tensor_tensor(
+                out=e[k][:, rows, :], in0=y2[:, rows].unsqueeze(2).to_broadcast([P, ROWS // 2, W]), scalar=-2.0,
+                in1=e[k][:, rows, :], op0=ALU.add, op1=ALU.mult,
+            )
+
+        def join(k, half):
+            rows = slice(half * ROWS // 2, (half + 1) * ROWS // 2)
+            nc.gpsimd.tensor_tensor(out=m1[k][:, rows, :], in0=m1[k][:, rows, :], in1=e[k][:, rows, :], op=ALU.add)
 
         def write_ds(k):
             tile_no = k // CHUNKS_PER_TILE
@@ -167,7 +182,7 @@ def tile_dendriticlayersilu_ffn_v_kernel(tc, x, template_flat, s, grad_out, out)
                 ds_grouped[tile_no] = two.tile([P, W, H_TILE, PACK], BF16, align_bytes=64, name="ds_grouped")
             f0 = (k % CHUNKS_PER_TILE) * H_CHUNK
             m1_v = m1[k][:].rearrange("p (j h) w -> p h w j", j=PACK)
-            c_v = c[k][:].rearrange("p j h -> p h j").unsqueeze(2).to_broadcast([P, H_CHUNK, 4, PACK])
+            c_v = back[k][:, 0:ROWS].rearrange("p (j h) -> p h j", j=PACK).unsqueeze(2).to_broadcast([P, H_CHUNK, 4, PACK])
             for w0 in range(0, W, 4):
                 nc.vector.tensor_tensor(
                     out=ds_grouped[tile_no][:, w0 : w0 + 4, f0 : f0 + H_CHUNK, :].rearrange("p w h j -> p h w j"),
@@ -230,48 +245,57 @@ def tile_dendriticlayersilu_ffn_v_kernel(tc, x, template_flat, s, grad_out, out)
                     first = (w - i) * K
                     nc.scalar.dma_start(out=out[rows, first : first + STORE_BANKS * K], in_=out_sb[:])
 
-        for r in range(CHUNKS + 3):
-            new = r if r < CHUNKS else None
-            mid = r - 1 if 0 <= r - 1 < CHUNKS else None
-            turn = r - 2 if 0 <= r - 2 < CHUNKS else None
-            old = r - 3 if r - 3 >= 0 else None
-            full = None
-            if old is not None and old > 0 and old % CHUNKS_PER_TILE == 0:
-                full = old // CHUNKS_PER_TILE - 1
+        for j in range(PACK):
+            nc.sync.dma_start(out=g_sb[:, :, j, :], in_=g_rows[:, j, :].rearrange("p (k h) -> p k h", h=H_CHUNK))
+        DEPTH = 5
+        ds_ready = None
+        for r in range(CHUNKS + DEPTH + 1):
+            def stage(lag):
+                return r - lag if 0 <= r - lag < CHUNKS else None
+
+            new, mid, turn, old, yk, dk = stage(0), stage(1), stage(2), stage(3), stage(4), stage(5)
+            full = ds_ready
+            ds_ready = None
             windows = list(range(r * X_PER_ROUND, min((r + 1) * X_PER_ROUND, W)))
 
-            if turn is not None:
-                turn_sums_back(turn)
             if new is not None:
                 load_s(new)
-                if new == 0:
-                    nc.sync.dma_start(out=g_sb[:], in_=g_rows)
                 tanh_and_silu(new)
+            if r == 0:
+                turn_grad_out()
             for w in windows:
                 load_x(w)
 
-            if old is not None:
-                newton_product(old)
+            if yk is not None:
+                weigh_mean(yk, 0)
+                join(yk, 0)
+                weigh_mean(yk, 1)
+                join(yk, 1)
             if new is not None:
                 maximum(new)
             if old is not None:
-                newton_step(old)
-            if mid is not None:
-                weigh_silu(mid)
-                add_windows(mid)
-            if full is not None:
-                ds_codes, ds_scales = quantise_ds(full)
+                newton_product(old)
+            if dk is not None:
+                write_ds(dk)
+                if dk % CHUNKS_PER_TILE == CHUNKS_PER_TILE - 1:
+                    ds_ready = dk // CHUNKS_PER_TILE
             if old is not None:
-                mean_and_factor(old)
-                weigh_mean(old)
+                newton_step(old)
             if new is not None:
                 shift(new)
             if old is not None:
-                join(old)
+                mean(old)
+            if mid is not None:
+                weigh_silu(mid)
+            if old is not None:
+                factor(old)
+                turn_back(old)
+            if mid is not None:
+                add_windows(mid)
+            if full is not None:
+                ds_codes, ds_scales = quantise_ds(full)
             if mid is not None:
                 weigh_tanh(mid)
-            if old is not None:
-                write_ds(old)
             for w in windows:
                 regroup_x(w)
                 if w - 1 in windows:
@@ -284,7 +308,5 @@ def tile_dendriticlayersilu_ffn_v_kernel(tc, x, template_flat, s, grad_out, out)
             if new is not None:
                 exponential(new)
             if full is not None:
-                multiply_and_store(full, ds_codes, ds_scales, [nc.scalar.copy])
-
-        ds_codes, ds_scales = quantise_ds(H // H_TILE - 1)
-        multiply_and_store(H // H_TILE - 1, ds_codes, ds_scales, [nc.scalar.copy, nc.vector.tensor_copy])
+                last = full == H // H_TILE - 1
+                multiply_and_store(full, ds_codes, ds_scales, [nc.scalar.copy, nc.vector.tensor_copy] if last else [nc.scalar.copy])

@@ -44,8 +44,8 @@ def tile_dendriticlayersilu_ffn_v_kernel(tc, x, template_flat, s, grad_out, out)
         stack.enter_context(tc.manual_schedule())
         keep = stack.enter_context(tc.tile_pool(name="keep", bufs=1))
         x_raw_pool = stack.enter_context(tc.tile_pool(name="x_raw", bufs=X_PER_ROUND))
-        six = stack.enter_context(tc.tile_pool(name="six", bufs=6))
         five = stack.enter_context(tc.tile_pool(name="five", bufs=5))
+        four = stack.enter_context(tc.tile_pool(name="four", bufs=4))
         three = stack.enter_context(tc.tile_pool(name="three", bufs=3))
         two = stack.enter_context(tc.tile_pool(name="two", bufs=2))
         sums_psum = stack.enter_context(tc.psum_pool(name="sums_psum", bufs=2))
@@ -62,7 +62,7 @@ def tile_dendriticlayersilu_ffn_v_kernel(tc, x, template_flat, s, grad_out, out)
 
         s_sb, top, e, m1, a1 = {}, {}, {}, {}, {}
         sums_t, back, guess, nrz, yc_t = {}, {}, {}, {}, {}
-        x_raw, x_grouped, ds_grouped = {}, {}, {}
+        x_raw, x_grouped, ds_grouped, quantised, out_sb = {}, {}, {}, {}, {}
 
         def spread(small):
             return small.unsqueeze(2).to_broadcast(wide)
@@ -79,7 +79,7 @@ def tile_dendriticlayersilu_ffn_v_kernel(tc, x, template_flat, s, grad_out, out)
             nc.sync.dma_start(out=x_raw[w][:], in_=x_rows[:, :, w * K : (w + 1) * K])
 
         def tanh_and_silu(k):
-            m1[k] = six.tile(wide, F32, name="m1")
+            m1[k] = five.tile(wide, F32, name="m1")
             nc.scalar.activation(out=m1[k][:], in_=s_sb[k][:], func=ACT.Tanh, scale=0.5)
             a1[k] = two.tile(wide, F32, name="a1")
             nc.scalar.activation(out=a1[k][:], in_=s_sb[k][:], func=ACT.Silu)
@@ -92,20 +92,21 @@ def tile_dendriticlayersilu_ffn_v_kernel(tc, x, template_flat, s, grad_out, out)
             nc.scalar.activation(out=guess[k][:], in_=sums_t[k][:, 0:ROWS], func=ACT.Ln)
             nc.scalar.activation(out=guess[k][:], in_=guess[k][:], func=ACT.Exp, scale=-1.0)
 
-        def add_windows(k):
-            sums_t[k] = sums_psum.tile([P, 2 * ROWS], F32, name="sums_t")
-            for i, terms in enumerate((e[k], a1[k])):
-                for b in range(BLOCKS):
-                    col = (i * BLOCKS + b) * P
-                    for w in range(W):
-                        nc.tensor.matmul(
-                            out=sums_t[k][:, col : col + P],
-                            lhsT=terms[:, b * P : (b + 1) * P, w],
-                            rhs=identity[:],
-                            is_transpose=True,
-                            start=(w == 0),
-                            stop=(w == W - 1),
-                        )
+        def add_windows(k, i):
+            if i == 0:
+                sums_t[k] = sums_psum.tile([P, 2 * ROWS], F32, name="sums_t")
+            terms = (e[k], a1[k])[i]
+            for b in range(BLOCKS):
+                col = (i * BLOCKS + b) * P
+                for w in range(W):
+                    nc.tensor.matmul(
+                        out=sums_t[k][:, col : col + P],
+                        lhsT=terms[:, b * P : (b + 1) * P, w],
+                        rhs=identity[:],
+                        is_transpose=True,
+                        start=(w == 0),
+                        stop=(w == W - 1),
+                    )
 
         def turn_back(k):
             back[k] = sums_psum.tile([P, 2 * ROWS], F32, name="back")
@@ -128,7 +129,7 @@ def tile_dendriticlayersilu_ffn_v_kernel(tc, x, template_flat, s, grad_out, out)
             nc.vector.tensor_reduce(out=top[k][:], in_=s_sb[k][:], axis=AXIS.X, op=ALU.max)
 
         def shift(k):
-            e[k] = five.tile(wide, F32, name="e")
+            e[k] = four.tile(wide, F32, name="e")
             nc.vector.tensor_tensor(out=e[k][:], in0=s_sb[k][:], in1=spread(top[k][:]), op=ALU.subtract)
 
         def weigh_silu(k):
@@ -141,19 +142,10 @@ def tile_dendriticlayersilu_ffn_v_kernel(tc, x, template_flat, s, grad_out, out)
                 out=m1[k][:], in0=m1[k][:], scalar=-3.0, in1=a1[k][:], op0=ALU.add, op1=ALU.mult
             )
 
-        def newton_product(k):
-            nrz[k] = two.tile([P, ROWS], F32, name="nrz")
-            nc.vector.tensor_tensor(out=nrz[k][:], in0=sums_t[k][:, 0:ROWS], in1=guess[k][:], op=ALU.mult)
-
-        def newton_step(k):
-            nc.vector.scalar_tensor_tensor(
-                out=nrz[k][:], in0=nrz[k][:], scalar=-2.0, in1=guess[k][:], op0=ALU.add, op1=ALU.mult
-            )
-
         def mean(k):
             yc_t[k] = two.tile([P, 2 * ROWS], F32, name="yc_t")
             nc.vector.scalar_tensor_tensor(
-                out=yc_t[k][:, ROWS : 2 * ROWS], in0=sums_t[k][:, ROWS : 2 * ROWS], scalar=-2.0, in1=nrz[k][:],
+                out=yc_t[k][:, ROWS : 2 * ROWS], in0=sums_t[k][:, ROWS : 2 * ROWS], scalar=2.0, in1=guess[k][:],
                 op0=ALU.mult, op1=ALU.mult,
             )
 
@@ -161,7 +153,7 @@ def tile_dendriticlayersilu_ffn_v_kernel(tc, x, template_flat, s, grad_out, out)
             nc.vector.scalar_tensor_tensor(
                 out=yc_t[k][:, 0:ROWS],
                 in0=g_t[:, k * BLOCKS : (k + 1) * BLOCKS, :].rearrange("p b q -> p (b q)"),
-                scalar=0.5, in1=nrz[k][:], op0=ALU.mult, op1=ALU.mult,
+                scalar=-0.5, in1=guess[k][:], op0=ALU.mult, op1=ALU.mult,
             )
 
         def weigh_mean(k, half):
@@ -215,14 +207,14 @@ def tile_dendriticlayersilu_ffn_v_kernel(tc, x, template_flat, s, grad_out, out)
                 in_=x_grouped[w][:].rearrange("p c j -> p (c j)"),
             )
 
-        def multiply_and_store(tile_no, ds_codes, ds_scales, copiers):
-            rows = slice(tile_no * H_TILE, (tile_no + 1) * H_TILE)
-            accs = []
+        accs = {}
 
-            def product(w):
-                acc = acc_psum.tile([H_TILE, K], F32, name="acc")
+        def products(tile_no, half):
+            ds_codes, ds_scales = quantised[tile_no]
+            for w in range(half * ACC_BANKS, (half + 1) * ACC_BANKS):
+                accs[w] = acc_psum.tile([H_TILE, K], F32, name="acc")
                 nc.tensor.matmul_mx(
-                    out=acc[:],
+                    out=accs[w][:],
                     lhsT=ds_codes[:, w, :].bitcast(E5M2_X4),
                     lhsT_scale=ds_scales[:, w, :],
                     rhs=x_codes[:, w, :].bitcast(E4M3_X4),
@@ -230,32 +222,30 @@ def tile_dendriticlayersilu_ffn_v_kernel(tc, x, template_flat, s, grad_out, out)
                     start=True,
                     stop=True,
                 )
-                accs.append(acc)
 
-            for w in range(ACC_BANKS):
-                product(w)
-            for w in range(W):
+        def empty_and_store(tile_no, half, copiers):
+            rows = slice(tile_no * H_TILE, (tile_no + 1) * H_TILE)
+            for w in range(half * ACC_BANKS, (half + 1) * ACC_BANKS):
                 i = w % STORE_BANKS
                 if i == 0:
-                    out_sb = three.tile([P, STORE_BANKS * K], F32, name="out_sb")
-                copiers[w % len(copiers)](out=out_sb[:, i * K : (i + 1) * K], in_=accs[w][:])
-                if w + ACC_BANKS < W:
-                    product(w + ACC_BANKS)
+                    out_sb[0] = three.tile([P, STORE_BANKS * K], F32, name="out_sb")
+                copiers[w % len(copiers)](out=out_sb[0][:, i * K : (i + 1) * K], in_=accs[w][:])
                 if i == STORE_BANKS - 1:
                     first = (w - i) * K
-                    nc.scalar.dma_start(out=out[rows, first : first + STORE_BANKS * K], in_=out_sb[:])
+                    nc.scalar.dma_start(out=out[rows, first : first + STORE_BANKS * K], in_=out_sb[0][:])
 
         for j in range(PACK):
             nc.sync.dma_start(out=g_sb[:, :, j, :], in_=g_rows[:, j, :].rearrange("p (k h) -> p k h", h=H_CHUNK))
-        DEPTH = 5
+        DEPTH = 4
         ds_ready = None
-        for r in range(CHUNKS + DEPTH + 1):
+        second = None
+        for r in range(CHUNKS + DEPTH + 3):
             def stage(lag):
                 return r - lag if 0 <= r - lag < CHUNKS else None
 
-            new, mid, turn, old, yk, dk = stage(0), stage(1), stage(2), stage(3), stage(4), stage(5)
-            full = ds_ready
-            ds_ready = None
+            new, mid, turn, old, dk = stage(0), stage(1), stage(2), stage(3), stage(4)
+            first_half, second_half = ds_ready, second
+            ds_ready, second = None, first_half
             windows = list(range(r * X_PER_ROUND, min((r + 1) * X_PER_ROUND, W)))
 
             if new is not None:
@@ -266,35 +256,25 @@ def tile_dendriticlayersilu_ffn_v_kernel(tc, x, template_flat, s, grad_out, out)
             for w in windows:
                 load_x(w)
 
-            if yk is not None:
-                weigh_mean(yk, 0)
-                join(yk, 0)
-                weigh_mean(yk, 1)
-                join(yk, 1)
             if new is not None:
                 maximum(new)
             if old is not None:
-                newton_product(old)
-            if dk is not None:
-                write_ds(dk)
-                if dk % CHUNKS_PER_TILE == CHUNKS_PER_TILE - 1:
-                    ds_ready = dk // CHUNKS_PER_TILE
-            if old is not None:
-                newton_step(old)
+                mean(old)
             if new is not None:
                 shift(new)
-            if old is not None:
-                mean(old)
-            if mid is not None:
-                weigh_silu(mid)
             if old is not None:
                 factor(old)
                 turn_back(old)
             if mid is not None:
-                add_windows(mid)
-            if full is not None:
-                ds_codes, ds_scales = quantise_ds(full)
+                weigh_silu(mid)
+            if second_half is not None:
+                products(second_half, 1)
+            if first_half is not None:
+                quantised[first_half] = quantise_ds(first_half)
+                products(first_half, 0)
             if mid is not None:
+                add_windows(mid, 0)
+                add_windows(mid, 1)
                 weigh_tanh(mid)
             for w in windows:
                 regroup_x(w)
@@ -302,11 +282,21 @@ def tile_dendriticlayersilu_ffn_v_kernel(tc, x, template_flat, s, grad_out, out)
                     quantise_x(w - 1)
             if windows:
                 quantise_x(windows[-1])
+            if old is not None:
+                weigh_mean(old, 0)
+                join(old, 0)
+                weigh_mean(old, 1)
+                join(old, 1)
+            if dk is not None:
+                write_ds(dk)
+                if dk % CHUNKS_PER_TILE == CHUNKS_PER_TILE - 1:
+                    ds_ready = dk // CHUNKS_PER_TILE
 
             if turn is not None:
                 guess_reciprocal(turn)
             if new is not None:
                 exponential(new)
-            if full is not None:
-                last = full == H // H_TILE - 1
-                multiply_and_store(full, ds_codes, ds_scales, [nc.scalar.copy, nc.vector.tensor_copy] if last else [nc.scalar.copy])
+            for tile_no, half in ((second_half, 1), (first_half, 0)):
+                if tile_no is not None:
+                    both = [nc.scalar.copy, nc.vector.tensor_copy] if tile_no == H // H_TILE - 1 else [nc.scalar.copy]
+                    empty_and_store(tile_no, half, both)

@@ -48,6 +48,7 @@ def tile_dendriticlayersilu_ffn_v_kernel(tc, x, template_flat, s, grad_out, out)
         four = stack.enter_context(tc.tile_pool(name="four", bufs=4))
         three = stack.enter_context(tc.tile_pool(name="three", bufs=3))
         two = stack.enter_context(tc.tile_pool(name="two", bufs=2))
+        out_pool = stack.enter_context(tc.tile_pool(name="out_pool", bufs=6))
         sums_psum = stack.enter_context(tc.psum_pool(name="sums_psum", bufs=2))
         acc_psum = stack.enter_context(tc.psum_pool(name="acc_psum", bufs=ACC_BANKS))
 
@@ -164,9 +165,9 @@ def tile_dendriticlayersilu_ffn_v_kernel(tc, x, template_flat, s, grad_out, out)
                 in1=e[k][:, rows, :], op0=ALU.add, op1=ALU.mult,
             )
 
-        def join(k, half):
+        def join(k, half, engine):
             rows = slice(half * ROWS // 2, (half + 1) * ROWS // 2)
-            nc.gpsimd.tensor_tensor(out=m1[k][:, rows, :], in0=m1[k][:, rows, :], in1=e[k][:, rows, :], op=ALU.add)
+            engine.tensor_tensor(out=m1[k][:, rows, :], in0=m1[k][:, rows, :], in1=e[k][:, rows, :], op=ALU.add)
 
         def write_ds(k):
             tile_no = k // CHUNKS_PER_TILE
@@ -183,15 +184,18 @@ def tile_dendriticlayersilu_ffn_v_kernel(tc, x, template_flat, s, grad_out, out)
                     op=ALU.mult,
                 )
 
-        def quantise_ds(tile_no):
-            ds_codes = two.tile([P, W, H_TILE], U32, align_bytes=64, name="ds_codes")
-            ds_scales = two.tile([P, W, H_TILE], U8, align_bytes=64, name="ds_scales")
+        def quantise_ds(tile_no, half):
+            if half == 0:
+                ds_codes = two.tile([P, W, H_TILE], U32, align_bytes=64, name="ds_codes")
+                ds_scales = two.tile([P, W, H_TILE], U8, align_bytes=64, name="ds_scales")
+                quantised[tile_no] = (ds_codes, ds_scales)
+            ds_codes, ds_scales = quantised[tile_no]
+            ws = slice(half * ACC_BANKS, (half + 1) * ACC_BANKS)
             nc.vector.quantize_mx(
-                out=ds_codes[:].rearrange("p w h -> p (w h)").bitcast(E5M2_X4),
-                scales=ds_scales[:].rearrange("p w h -> p (w h)"),
-                in_=ds_grouped[tile_no][:].rearrange("p w h j -> p (w h j)"),
+                out=ds_codes[:, ws, :].rearrange("p w h -> p (w h)").bitcast(E5M2_X4),
+                scales=ds_scales[:, ws, :].rearrange("p w h -> p (w h)"),
+                in_=ds_grouped[tile_no][:, ws, :, :].rearrange("p w h j -> p (w h j)"),
             )
-            return ds_codes, ds_scales
 
         def regroup_x(w):
             x_grouped[w] = two.tile([P, K, PACK], BF16, align_bytes=64, name="x_grouped")
@@ -228,14 +232,12 @@ def tile_dendriticlayersilu_ffn_v_kernel(tc, x, template_flat, s, grad_out, out)
             for w in range(half * ACC_BANKS, (half + 1) * ACC_BANKS):
                 i = w % STORE_BANKS
                 if i == 0:
-                    out_sb[0] = three.tile([P, STORE_BANKS * K], F32, name="out_sb")
+                    out_sb[0] = out_pool.tile([P, STORE_BANKS * K], F32, name="out_sb")
                 copiers[w % len(copiers)](out=out_sb[0][:, i * K : (i + 1) * K], in_=accs[w][:])
                 if i == STORE_BANKS - 1:
                     first = (w - i) * K
                     nc.scalar.dma_start(out=out[rows, first : first + STORE_BANKS * K], in_=out_sb[0][:])
 
-        for j in range(PACK):
-            nc.sync.dma_start(out=g_sb[:, :, j, :], in_=g_rows[:, j, :].rearrange("p (k h) -> p k h", h=H_CHUNK))
         DEPTH = 4
         ds_ready = None
         second = None
@@ -252,6 +254,8 @@ def tile_dendriticlayersilu_ffn_v_kernel(tc, x, template_flat, s, grad_out, out)
                 load_s(new)
                 tanh_and_silu(new)
             if r == 0:
+                for j in range(PACK):
+                    nc.sync.dma_start(out=g_sb[:, :, j, :], in_=g_rows[:, j, :].rearrange("p (k h) -> p k h", h=H_CHUNK))
                 turn_grad_out()
             for w in windows:
                 load_x(w)
@@ -262,16 +266,20 @@ def tile_dendriticlayersilu_ffn_v_kernel(tc, x, template_flat, s, grad_out, out)
                 mean(old)
             if new is not None:
                 shift(new)
+            if mid is not None:
+                weigh_silu(mid)
             if old is not None:
                 factor(old)
                 turn_back(old)
-            if mid is not None:
-                weigh_silu(mid)
-            if second_half is not None:
+            LAST = H // H_TILE - 1
+            if second_half is not None and second_half != LAST:
+                quantise_ds(second_half, 1)
                 products(second_half, 1)
             if first_half is not None:
-                quantised[first_half] = quantise_ds(first_half)
+                quantise_ds(first_half, 0)
                 products(first_half, 0)
+                if first_half == LAST:
+                    quantise_ds(first_half, 1)
             if mid is not None:
                 add_windows(mid, 0)
                 add_windows(mid, 1)
@@ -282,21 +290,29 @@ def tile_dendriticlayersilu_ffn_v_kernel(tc, x, template_flat, s, grad_out, out)
                     quantise_x(w - 1)
             if windows:
                 quantise_x(windows[-1])
+            long_window = dk is not None and r + 1 < CHUNKS
             if old is not None:
                 weigh_mean(old, 0)
-                join(old, 0)
+                join(old, 0, nc.gpsimd)
                 weigh_mean(old, 1)
-                join(old, 1)
+                if long_window:
+                    join(old, 1, nc.gpsimd)
             if dk is not None:
                 write_ds(dk)
                 if dk % CHUNKS_PER_TILE == CHUNKS_PER_TILE - 1:
                     ds_ready = dk // CHUNKS_PER_TILE
+            if old is not None and not long_window:
+                join(old, 1, nc.vector)
 
             if turn is not None:
                 guess_reciprocal(turn)
             if new is not None:
                 exponential(new)
-            for tile_no, half in ((second_half, 1), (first_half, 0)):
-                if tile_no is not None:
-                    both = [nc.scalar.copy, nc.vector.tensor_copy] if tile_no == H // H_TILE - 1 else [nc.scalar.copy]
-                    empty_and_store(tile_no, half, both)
+            if second_half is not None and second_half != LAST:
+                empty_and_store(second_half, 1, [nc.scalar.copy])
+            if first_half is not None and first_half != LAST:
+                empty_and_store(first_half, 0, [nc.scalar.copy])
+            if first_half == LAST:
+                empty_and_store(LAST, 0, [nc.scalar.copy, nc.vector.tensor_copy])
+                products(LAST, 1)
+                empty_and_store(LAST, 1, [nc.scalar.copy, nc.vector.tensor_copy])

@@ -27,6 +27,7 @@ ROWS = PACK * H_CHUNK
 BLOCKS = ROWS // P
 ACC_BANKS = 4
 STORE_BANKS = 2
+X_ON_SCALAR = (5, 7)
 X_PER_ROUND = 3
 
 FLOPS = 2 * TOKENS * H * W * K
@@ -197,9 +198,9 @@ def tile_dendriticlayersilu_ffn_v_kernel(tc, x, template_flat, s, grad_out, out)
                 in_=ds_grouped[tile_no][:, ws, :, :].rearrange("p w h j -> p (w h j)"),
             )
 
-        def regroup_x(w):
-            x_grouped[w] = two.tile([P, K, PACK], BF16, align_bytes=64, name="x_grouped")
-            nc.vector.tensor_copy(
+        def regroup_x(w, copier):
+            x_grouped[w] = three.tile([P, K, PACK], BF16, align_bytes=64, name="x_grouped")
+            copier(
                 out=x_grouped[w][:].rearrange("p (c i) j -> p c j i", i=4),
                 in_=x_raw[w][:].rearrange("p j (c i) -> p c j i", i=4),
             )
@@ -241,6 +242,7 @@ def tile_dendriticlayersilu_ffn_v_kernel(tc, x, template_flat, s, grad_out, out)
         DEPTH = 4
         ds_ready = None
         second = None
+        late = []
         for r in range(CHUNKS + DEPTH + 3):
             def stage(lag):
                 return r - lag if 0 <= r - lag < CHUNKS else None
@@ -284,12 +286,16 @@ def tile_dendriticlayersilu_ffn_v_kernel(tc, x, template_flat, s, grad_out, out)
                 add_windows(mid, 0)
                 add_windows(mid, 1)
                 weigh_tanh(mid)
-            for w in windows:
-                regroup_x(w)
-                if w - 1 in windows:
+            for w in late:
+                quantise_x(w)
+            late = [w for w in windows if w in X_ON_SCALAR]
+            mine = [w for w in windows if w not in X_ON_SCALAR]
+            for w in mine:
+                regroup_x(w, nc.vector.tensor_copy)
+                if w - 1 in mine:
                     quantise_x(w - 1)
-            if windows:
-                quantise_x(windows[-1])
+            if mine:
+                quantise_x(mine[-1])
             long_window = dk is not None and r + 1 < CHUNKS
             if old is not None:
                 weigh_mean(old, 0)
@@ -308,6 +314,8 @@ def tile_dendriticlayersilu_ffn_v_kernel(tc, x, template_flat, s, grad_out, out)
                 guess_reciprocal(turn)
             if new is not None:
                 exponential(new)
+            for w in late:
+                regroup_x(w, nc.scalar.copy)
             if second_half is not None and second_half != LAST:
                 empty_and_store(second_half, 1, [nc.scalar.copy])
             if first_half is not None and first_half != LAST:

@@ -124,7 +124,7 @@ def tile_dendriticlayersilu_ffn_v_kernel(tc, x, template_flat, s, grad_out, out)
                     rows = g_sb[:, k, :, :].rearrange("p j h -> p (j h)")
                     nc.tensor.transpose(out=g_ps[:, i, :], in_=rows[:, b * P : (b + 1) * P], identity=identity_bf[:])
                 n = CHUNKS * BLOCKS // 2
-                nc.scalar.copy(out=g_t[:, half * n : (half + 1) * n, :], in_=g_ps[:])
+                nc.scalar.mul(out=g_t[:, half * n : (half + 1) * n, :], in_=g_ps[:], mul=-0.5)
 
         def maximum(k):
             top[k] = two.tile([P, ROWS], F32, name="top")
@@ -145,17 +145,17 @@ def tile_dendriticlayersilu_ffn_v_kernel(tc, x, template_flat, s, grad_out, out)
             )
 
         def mean(k):
-            yc_t[k] = two.tile([P, 2 * ROWS], F32, name="yc_t")
             nc.vector.scalar_tensor_tensor(
                 out=yc_t[k][:, ROWS : 2 * ROWS], in0=sums_t[k][:, ROWS : 2 * ROWS], scalar=2.0, in1=guess[k][:],
                 op0=ALU.mult, op1=ALU.mult,
             )
 
         def factor(k):
-            nc.vector.scalar_tensor_tensor(
+            yc_t[k] = three.tile([P, 2 * ROWS], F32, name="yc_t")
+            nc.gpsimd.tensor_tensor(
                 out=yc_t[k][:, 0:ROWS],
                 in0=g_t[:, k * BLOCKS : (k + 1) * BLOCKS, :].rearrange("p b q -> p (b q)"),
-                scalar=-0.5, in1=guess[k][:], op0=ALU.mult, op1=ALU.mult,
+                in1=guess[k][:], op=ALU.mult,
             )
 
         def weigh_mean(k, half):
@@ -266,13 +266,11 @@ def tile_dendriticlayersilu_ffn_v_kernel(tc, x, template_flat, s, grad_out, out)
                 maximum(new)
             if old is not None:
                 mean(old)
-            if new is not None:
-                shift(new)
+                turn_back(old)
             if mid is not None:
                 weigh_silu(mid)
-            if old is not None:
-                factor(old)
-                turn_back(old)
+            if new is not None:
+                shift(new)
             LAST = H // H_TILE - 1
             if second_half is not None and second_half != LAST:
                 quantise_ds(second_half, 1)
@@ -312,6 +310,7 @@ def tile_dendriticlayersilu_ffn_v_kernel(tc, x, template_flat, s, grad_out, out)
 
             if turn is not None:
                 guess_reciprocal(turn)
+                factor(turn)
             if new is not None:
                 exponential(new)
             for w in late:

@@ -71,20 +71,22 @@ def tile_dendriticlayersilu_ffn_v_kernel(tc, x, template_flat, s, grad_out, out)
 
         def load_s(k):
             s_sb[k] = three.tile([P, ROWS, W], F32, name="s_sb")
-            nc.sync.dma_start(
-                out=s_sb[k][:].rearrange("p (j h) w -> p j h w", j=PACK),
-                in_=s_rows[:, :, k * H_CHUNK : (k + 1) * H_CHUNK, :],
-            )
+            features = slice(k * H_CHUNK, (k + 1) * H_CHUNK)
+            if k == 0:
+                for j in range(PACK):
+                    nc.sync.dma_start(out=s_sb[k][:, j * H_CHUNK : (j + 1) * H_CHUNK, :], in_=s_rows[:, j, features, :])
+            else:
+                nc.sync.dma_start(out=s_sb[k][:].rearrange("p (j h) w -> p j h w", j=PACK), in_=s_rows[:, :, features, :])
 
         def load_x(w):
             x_raw[w] = x_raw_pool.tile([P, PACK, K], BF16, name="x_raw")
             nc.sync.dma_start(out=x_raw[w][:], in_=x_rows[:, :, w * K : (w + 1) * K])
 
         def tanh_and_silu(k):
-            m1[k] = five.tile(wide, F32, name="m1")
-            nc.scalar.activation(out=m1[k][:], in_=s_sb[k][:], func=ACT.Tanh, scale=0.5)
             a1[k] = two.tile(wide, F32, name="a1")
             nc.scalar.activation(out=a1[k][:], in_=s_sb[k][:], func=ACT.Silu)
+            m1[k] = five.tile(wide, F32, name="m1")
+            nc.scalar.activation(out=m1[k][:], in_=s_sb[k][:], func=ACT.Tanh, scale=0.5)
 
         def exponential(k):
             nc.scalar.activation(out=e[k][:], in_=e[k][:], func=ACT.Exp)
@@ -128,7 +130,10 @@ def tile_dendriticlayersilu_ffn_v_kernel(tc, x, template_flat, s, grad_out, out)
 
         def maximum(k):
             top[k] = two.tile([P, ROWS], F32, name="top")
-            nc.vector.tensor_reduce(out=top[k][:], in_=s_sb[k][:], axis=AXIS.X, op=ALU.max)
+            pieces = PACK if k == 0 else 1
+            for i in range(pieces):
+                rows = slice(i * ROWS // pieces, (i + 1) * ROWS // pieces)
+                nc.vector.tensor_reduce(out=top[k][:, rows], in_=s_sb[k][:, rows, :], axis=AXIS.X, op=ALU.max)
 
         def shift(k):
             e[k] = four.tile(wide, F32, name="e")
@@ -235,7 +240,9 @@ def tile_dendriticlayersilu_ffn_v_kernel(tc, x, template_flat, s, grad_out, out)
                 if i == 0:
                     out_sb[0] = out_pool.tile([P, STORE_BANKS * K], F32, name="out_sb")
                 copiers[w % len(copiers)](out=out_sb[0][:, i * K : (i + 1) * K], in_=accs[w][:])
-                if i == STORE_BANKS - 1:
+                if len(copiers) > 1:
+                    nc.sync.dma_start(out=out[rows, w * K : (w + 1) * K], in_=out_sb[0][:, i * K : (i + 1) * K])
+                elif i == STORE_BANKS - 1:
                     first = (w - i) * K
                     nc.scalar.dma_start(out=out[rows, first : first + STORE_BANKS * K], in_=out_sb[0][:])
 
@@ -258,7 +265,6 @@ def tile_dendriticlayersilu_ffn_v_kernel(tc, x, template_flat, s, grad_out, out)
             if r == 0:
                 for j in range(PACK):
                     nc.sync.dma_start(out=g_sb[:, :, j, :], in_=g_rows[:, j, :].rearrange("p (k h) -> p k h", h=H_CHUNK))
-                turn_grad_out()
             for w in windows:
                 load_x(w)
 
@@ -313,6 +319,8 @@ def tile_dendriticlayersilu_ffn_v_kernel(tc, x, template_flat, s, grad_out, out)
                 factor(turn)
             if new is not None:
                 exponential(new)
+            if r == 0:
+                turn_grad_out()
             for w in late:
                 regroup_x(w, nc.scalar.copy)
             if second_half is not None and second_half != LAST:

@@ -82,9 +82,11 @@ def tile_dendriticlayersilu_ffn_v_kernel(tc, x, template_flat, s, grad_out, out)
             x_raw[w] = x_raw_pool.tile([P, PACK, K], BF16, name="x_raw")
             nc.sync.dma_start(out=x_raw[w][:], in_=x_rows[:, :, w * K : (w + 1) * K])
 
-        def tanh_and_silu(k):
-            a1[k] = two.tile(wide, F32, name="a1")
+        def silu(k):
+            a1[k] = three.tile(wide, F32, name="a1")
             nc.scalar.activation(out=a1[k][:], in_=s_sb[k][:], func=ACT.Silu)
+
+        def tanh(k):
             m1[k] = five.tile(wide, F32, name="m1")
             nc.scalar.activation(out=m1[k][:], in_=s_sb[k][:], func=ACT.Tanh, scale=0.5)
 
@@ -259,14 +261,20 @@ def tile_dendriticlayersilu_ffn_v_kernel(tc, x, template_flat, s, grad_out, out)
             ds_ready, second = None, first_half
             windows = list(range(r * X_PER_ROUND, min((r + 1) * X_PER_ROUND, W)))
 
-            if new is not None:
-                load_s(new)
-                tanh_and_silu(new)
+            if r == 0:
+                load_s(0)
+                load_x(0)
+            if r + 1 < CHUNKS:
+                load_s(r + 1)
+            if new is not None and r % 2 == 0:
+                silu(new)
+                silu(new + 1)
             if r == 0:
                 for j in range(PACK):
                     nc.sync.dma_start(out=g_sb[:, :, j, :], in_=g_rows[:, j, :].rearrange("p (k h) -> p k h", h=H_CHUNK))
             for w in windows:
-                load_x(w)
+                if w > 0:
+                    load_x(w)
 
             if new is not None:
                 maximum(new)
@@ -318,6 +326,7 @@ def tile_dendriticlayersilu_ffn_v_kernel(tc, x, template_flat, s, grad_out, out)
                 guess_reciprocal(turn)
                 factor(turn)
             if new is not None:
+                tanh(new)
                 exponential(new)
             if r == 0:
                 turn_grad_out()

@@ -27,7 +27,8 @@ ROWS = PACK * H_CHUNK
 BLOCKS = ROWS // P
 ACC_BANKS = 4
 STORE_BANKS = 2
-X_ON_SCALAR = (5, 7)
+X_PLAN = ((0, 1, 2), (3,), (4,), (5,), (6,), (7,))
+X_ON_SCALAR = (4, 5, 6, 7)
 X_PER_ROUND = 3
 
 FLOPS = 2 * TOKENS * H * W * K
@@ -259,7 +260,7 @@ def tile_dendriticlayersilu_ffn_v_kernel(tc, x, template_flat, s, grad_out, out)
             new, mid, turn, old, dk = stage(0), stage(1), stage(2), stage(3), stage(4)
             first_half, second_half = ds_ready, second
             ds_ready, second = None, first_half
-            windows = list(range(r * X_PER_ROUND, min((r + 1) * X_PER_ROUND, W)))
+            windows = list(X_PLAN[r]) if r < len(X_PLAN) else []
 
             if r == 0:
                 load_s(0)

@@ -183,12 +183,12 @@ def tile_dendriticlayersilu_ffn_v_kernel(tc, x, template_flat, s, grad_out, out)
             if k % CHUNKS_PER_TILE == 0:
                 ds_grouped[tile_no] = two.tile([P, W, H_TILE, PACK], BF16, align_bytes=64, name="ds_grouped")
             f0 = (k % CHUNKS_PER_TILE) * H_CHUNK
-            m1_v = m1[k][:].rearrange("p (j h) w -> p h w j", j=PACK)
-            c_v = back[k][:, 0:ROWS].rearrange("p (j h) -> p h j", j=PACK).unsqueeze(2).to_broadcast([P, H_CHUNK, 4, PACK])
+            m1_v = m1[k][:].rearrange("p (j h) w -> p h j w", j=PACK)
+            c_v = back[k][:, 0:ROWS].rearrange("p (j h) -> p h j", j=PACK).unsqueeze(3).to_broadcast([P, H_CHUNK, PACK, 4])
             for w0 in range(0, W, 4):
                 nc.vector.tensor_tensor(
-                    out=ds_grouped[tile_no][:, w0 : w0 + 4, f0 : f0 + H_CHUNK, :].rearrange("p w h j -> p h w j"),
-                    in0=m1_v[:, :, w0 : w0 + 4, :],
+                    out=ds_grouped[tile_no][:, w0 : w0 + 4, f0 : f0 + H_CHUNK, :].rearrange("p w h j -> p h j w"),
+                    in0=m1_v[:, :, :, w0 : w0 + 4],
                     in1=c_v,
                     op=ALU.mult,
                 )

@@ -25,12 +25,15 @@ CHUNKS = H // H_CHUNK
 CHUNKS_PER_TILE = H_TILE // H_CHUNK
 ROWS = PACK * H_CHUNK
 BLOCKS = ROWS // P
-ACC_BANKS = 4
+HALF_WINDOWS = 4
+ACC_BANKS = 3
 STORE_BANKS = 2
-X_PLAN = ((0, 1, 2), (3,), (4,), (5,), (6,), (7,))
-X_ON_SCALAR = (4, 5, 6, 7)
+X_PLAN = ((0,1,2),(3,4),(),(5,),(),(6,7))
+X_ON_SCALAR = (5,6,7)
 X_PER_ROUND = 3
 
+FIRST = 80
+SHIFT_ON_GPSIMD = 0
 FLOPS = 2 * TOKENS * H * W * K
 BYTES = TOKENS * W * K * 2 + TOKENS * H * W * 4 + TOKENS * H * 2 + H * W * K * 4
 
@@ -45,12 +48,13 @@ def tile_dendriticlayersilu_ffn_v_kernel(tc, x, template_flat, s, grad_out, out)
     with ExitStack() as stack:
         stack.enter_context(tc.manual_schedule())
         keep = stack.enter_context(tc.tile_pool(name="keep", bufs=1))
-        x_raw_pool = stack.enter_context(tc.tile_pool(name="x_raw", bufs=X_PER_ROUND))
+        x_raw_pool = stack.enter_context(tc.tile_pool(name="x_raw", bufs=3))
         five = stack.enter_context(tc.tile_pool(name="five", bufs=5))
         four = stack.enter_context(tc.tile_pool(name="four", bufs=4))
         three = stack.enter_context(tc.tile_pool(name="three", bufs=3))
         two = stack.enter_context(tc.tile_pool(name="two", bufs=2))
-        out_pool = stack.enter_context(tc.tile_pool(name="out_pool", bufs=6))
+        out_pool = stack.enter_context(tc.tile_pool(name="out_pool", bufs=4))
+        z_psum = stack.enter_context(tc.psum_pool(name="z_psum", bufs=1))
         sums_psum = stack.enter_context(tc.psum_pool(name="sums_psum", bufs=2))
         acc_psum = stack.enter_context(tc.psum_pool(name="acc_psum", bufs=ACC_BANKS))
 
@@ -63,8 +67,12 @@ def tile_dendriticlayersilu_ffn_v_kernel(tc, x, template_flat, s, grad_out, out)
         x_codes = keep.tile([P, W, K], U32, align_bytes=64)
         x_scales = keep.tile([P, W, K], U8, align_bytes=64)
 
+        warm = keep.tile([P, 1], F32)
+        nc.gpsimd.memset(warm[:], 0.0)
+        nc.scalar.activation(out=warm[:], in_=warm[:], func=ACT.Silu)
+
         s_sb, top, e, m1, a1 = {}, {}, {}, {}, {}
-        sums_t, back, guess, nrz, yc_t = {}, {}, {}, {}, {}
+        z_t, sums_t, back, guess, yc_t = {}, {}, {}, {}, {}
         x_raw, x_grouped, ds_grouped, quantised, out_sb = {}, {}, {}, {}, {}
 
         def spread(small):
@@ -94,26 +102,33 @@ def tile_dendriticlayersilu_ffn_v_kernel(tc, x, template_flat, s, grad_out, out)
         def exponential(k):
             nc.scalar.activation(out=e[k][:], in_=e[k][:], func=ACT.Exp)
 
-        def guess_reciprocal(k):
-            guess[k] = two.tile([P, ROWS], F32, name="guess")
-            nc.scalar.activation(out=guess[k][:], in_=sums_t[k][:, 0:ROWS], func=ACT.Ln)
-            nc.scalar.activation(out=guess[k][:], in_=guess[k][:], func=ACT.Exp, scale=-1.0)
+        def guess_reciprocals(k):
+            pair = two.tile([P, 2 * ROWS], F32, name="guess")
+            nc.scalar.activation(out=pair[:], in_=z_t[0][:], func=ACT.Ln)
+            nc.scalar.activation(out=pair[:], in_=pair[:], func=ACT.Exp, scale=-1.0)
+            guess[k], guess[k + 1] = pair[:, 0:ROWS], pair[:, ROWS : 2 * ROWS]
 
-        def add_windows(k, i):
-            if i == 0:
-                sums_t[k] = sums_psum.tile([P, 2 * ROWS], F32, name="sums_t")
-            terms = (e[k], a1[k])[i]
+        def add_windows(sums, terms):
             for b in range(BLOCKS):
-                col = (i * BLOCKS + b) * P
                 for w in range(W):
                     nc.tensor.matmul(
-                        out=sums_t[k][:, col : col + P],
+                        out=sums[:, b * P : (b + 1) * P],
                         lhsT=terms[:, b * P : (b + 1) * P, w],
                         rhs=identity[:],
                         is_transpose=True,
                         start=(w == 0),
                         stop=(w == W - 1),
                     )
+
+        def add_z(k):
+            if k % 2 == 0:
+                z_t[0] = z_psum.tile([P, 2 * ROWS], F32, name="z_t")
+            half = (k % 2) * ROWS
+            add_windows(z_t[0][:, half : half + ROWS], e[k])
+
+        def add_y(k):
+            sums_t[k] = sums_psum.tile([P, 2 * ROWS], F32, name="sums_t")
+            add_windows(sums_t[k][:, 0:ROWS], a1[k])
 
         def turn_back(k):
             back[k] = sums_psum.tile([P, 2 * ROWS], F32, name="back")
@@ -138,9 +153,14 @@ def tile_dendriticlayersilu_ffn_v_kernel(tc, x, template_flat, s, grad_out, out)
                 rows = slice(i * ROWS // pieces, (i + 1) * ROWS // pieces)
                 nc.vector.tensor_reduce(out=top[k][:, rows], in_=s_sb[k][:, rows, :], axis=AXIS.X, op=ALU.max)
 
-        def shift(k):
-            e[k] = four.tile(wide, F32, name="e")
-            nc.vector.tensor_tensor(out=e[k][:], in0=s_sb[k][:], in1=spread(top[k][:]), op=ALU.subtract)
+        def shift(k, engine, r0, r1):
+            if k not in e:
+                e[k] = four.tile(wide, F32, name="e")
+            if r0 < r1:
+                engine.tensor_tensor(
+                    out=e[k][:, r0:r1, :], in0=s_sb[k][:, r0:r1, :],
+                    in1=top[k][:, r0:r1].unsqueeze(2).to_broadcast([P, r1 - r0, W]), op=ALU.subtract,
+                )
 
         def weigh_silu(k):
             nc.vector.scalar_tensor_tensor(
@@ -154,7 +174,7 @@ def tile_dendriticlayersilu_ffn_v_kernel(tc, x, template_flat, s, grad_out, out)
 
         def mean(k):
             nc.vector.scalar_tensor_tensor(
-                out=yc_t[k][:, ROWS : 2 * ROWS], in0=sums_t[k][:, ROWS : 2 * ROWS], scalar=2.0, in1=guess[k][:],
+                out=yc_t[k][:, ROWS : 2 * ROWS], in0=sums_t[k][:, 0:ROWS], scalar=2.0, in1=guess[k],
                 op0=ALU.mult, op1=ALU.mult,
             )
 
@@ -163,47 +183,47 @@ def tile_dendriticlayersilu_ffn_v_kernel(tc, x, template_flat, s, grad_out, out)
             nc.gpsimd.tensor_tensor(
                 out=yc_t[k][:, 0:ROWS],
                 in0=g_t[:, k * BLOCKS : (k + 1) * BLOCKS, :].rearrange("p b q -> p (b q)"),
-                in1=guess[k][:], op=ALU.mult,
+                in1=guess[k], op=ALU.mult,
             )
 
-        def weigh_mean(k, half):
-            rows = slice(half * ROWS // 2, (half + 1) * ROWS // 2)
+        def weigh_mean(k, r0, r1):
+            rows = slice(r0, r1)
             y2 = back[k][:, ROWS : 2 * ROWS]
             nc.vector.scalar_tensor_tensor(
-                out=e[k][:, rows, :], in0=y2[:, rows].unsqueeze(2).to_broadcast([P, ROWS // 2, W]), scalar=-2.0,
+                out=e[k][:, rows, :], in0=y2[:, rows].unsqueeze(2).to_broadcast([P, r1 - r0, W]), scalar=-2.0,
                 in1=e[k][:, rows, :], op0=ALU.add, op1=ALU.mult,
             )
 
-        def join(k, half, engine):
-            rows = slice(half * ROWS // 2, (half + 1) * ROWS // 2)
-            engine.tensor_tensor(out=m1[k][:, rows, :], in0=m1[k][:, rows, :], in1=e[k][:, rows, :], op=ALU.add)
+        def join(k, r0, r1, engine):
+            rows = slice(r0, r1)
+            if r0 < r1:
+                engine.tensor_tensor(out=m1[k][:, rows, :], in0=m1[k][:, rows, :], in1=e[k][:, rows, :], op=ALU.add)
 
-        def write_ds(k):
+        def write_ds(k, pieces=((0, 4), (4, 8))):
             tile_no = k // CHUNKS_PER_TILE
             if k % CHUNKS_PER_TILE == 0:
                 ds_grouped[tile_no] = two.tile([P, W, H_TILE, PACK], BF16, align_bytes=64, name="ds_grouped")
             f0 = (k % CHUNKS_PER_TILE) * H_CHUNK
             m1_v = m1[k][:].rearrange("p (j h) w -> p h j w", j=PACK)
-            c_v = back[k][:, 0:ROWS].rearrange("p (j h) -> p h j", j=PACK).unsqueeze(3).to_broadcast([P, H_CHUNK, PACK, 4])
-            for w0 in range(0, W, 4):
+            for w0, w1 in pieces:
+                c_v = back[k][:, 0:ROWS].rearrange("p (j h) -> p h j", j=PACK).unsqueeze(3).to_broadcast([P, H_CHUNK, PACK, w1 - w0])
                 nc.vector.tensor_tensor(
-                    out=ds_grouped[tile_no][:, w0 : w0 + 4, f0 : f0 + H_CHUNK, :].rearrange("p w h j -> p h j w"),
-                    in0=m1_v[:, :, :, w0 : w0 + 4],
+                    out=ds_grouped[tile_no][:, w0:w1, f0 : f0 + H_CHUNK, :].rearrange("p w h j -> p h j w"),
+                    in0=m1_v[:, :, :, w0:w1],
                     in1=c_v,
                     op=ALU.mult,
                 )
 
-        def quantise_ds(tile_no, half):
-            if half == 0:
+        def quantise_ds(tile_no, w0, w1):
+            if w0 == 0:
                 ds_codes = two.tile([P, W, H_TILE], U32, align_bytes=64, name="ds_codes")
                 ds_scales = two.tile([P, W, H_TILE], U8, align_bytes=64, name="ds_scales")
                 quantised[tile_no] = (ds_codes, ds_scales)
             ds_codes, ds_scales = quantised[tile_no]
-            ws = slice(half * ACC_BANKS, (half + 1) * ACC_BANKS)
             nc.vector.quantize_mx(
-                out=ds_codes[:, ws, :].rearrange("p w h -> p (w h)").bitcast(E5M2_X4),
-                scales=ds_scales[:, ws, :].rearrange("p w h -> p (w h)"),
-                in_=ds_grouped[tile_no][:, ws, :, :].rearrange("p w h j -> p (w h j)"),
+                out=ds_codes[:, w0:w1, :].rearrange("p w h -> p (w h)").bitcast(E5M2_X4),
+                scales=ds_scales[:, w0:w1, :].rearrange("p w h -> p (w h)"),
+                in_=ds_grouped[tile_no][:, w0:w1, :, :].rearrange("p w h j -> p (w h j)"),
             )
 
         def regroup_x(w, copier):
@@ -222,10 +242,12 @@ def tile_dendriticlayersilu_ffn_v_kernel(tc, x, template_flat, s, grad_out, out)
 
         accs = {}
 
-        def products(tile_no, half):
+        def products(tile_no, w0, w1, spare=False):
             ds_codes, ds_scales = quantised[tile_no]
-            for w in range(half * ACC_BANKS, (half + 1) * ACC_BANKS):
-                accs[w] = acc_psum.tile([H_TILE, K], F32, name="acc")
+            all_banks = [(acc_psum, "acc")] * ACC_BANKS + [(z_psum, "z_t")] + [(sums_psum, "sums_t")] * 2 + [(sums_psum, "back")] * 2
+            for w in range(w0, w1):
+                pool, tag = all_banks[w] if spare else (acc_psum, "acc")
+                accs[w] = pool.tile([H_TILE, K], F32, name=tag)
                 nc.tensor.matmul_mx(
                     out=accs[w][:],
                     lhsT=ds_codes[:, w, :].bitcast(E5M2_X4),
@@ -236,68 +258,77 @@ def tile_dendriticlayersilu_ffn_v_kernel(tc, x, template_flat, s, grad_out, out)
                     stop=True,
                 )
 
-        def empty_and_store(tile_no, half, copiers):
+        def empty_and_store(tile_no, w0, w1, copiers, single=False):
             rows = slice(tile_no * H_TILE, (tile_no + 1) * H_TILE)
-            for w in range(half * ACC_BANKS, (half + 1) * ACC_BANKS):
+            for w in range(w0, w1):
                 i = w % STORE_BANKS
                 if i == 0:
                     out_sb[0] = out_pool.tile([P, STORE_BANKS * K], F32, name="out_sb")
                 copiers[w % len(copiers)](out=out_sb[0][:, i * K : (i + 1) * K], in_=accs[w][:])
-                if len(copiers) > 1:
+                if single:
                     nc.sync.dma_start(out=out[rows, w * K : (w + 1) * K], in_=out_sb[0][:, i * K : (i + 1) * K])
                 elif i == STORE_BANKS - 1:
                     first = (w - i) * K
-                    nc.scalar.dma_start(out=out[rows, first : first + STORE_BANKS * K], in_=out_sb[0][:])
+                    nc.sync.dma_start(out=out[rows, first : first + STORE_BANKS * K], in_=out_sb[0][:])
 
-        DEPTH = 4
-        ds_ready = None
-        second = None
         late = []
-        for r in range(CHUNKS + DEPTH + 3):
+        pend = []
+        LAST = H // H_TILE - 1
+        for r in range(CHUNKS + 6):
             def stage(lag):
                 return r - lag if 0 <= r - lag < CHUNKS else None
 
-            new, mid, turn, old, dk = stage(0), stage(1), stage(2), stage(3), stage(4)
-            first_half, second_half = ds_ready, second
-            ds_ready, second = None, first_half
+            new, mid, mk, yk, wk = stage(0), stage(1), stage(3), stage(4), stage(5)
             windows = list(X_PLAN[r]) if r < len(X_PLAN) else []
-
             if r == 0:
                 load_s(0)
-                load_x(0)
             if r + 1 < CHUNKS:
                 load_s(r + 1)
-            if new is not None and r % 2 == 0:
-                silu(new)
-                silu(new + 1)
             if r == 0:
-                for j in range(PACK):
-                    nc.sync.dma_start(out=g_sb[:, :, j, :], in_=g_rows[:, j, :].rearrange("p (k h) -> p k h", h=H_CHUNK))
+                load_x(0)
             for w in windows:
                 if w > 0:
                     load_x(w)
+            if r == 0:
+                for j in range(PACK):
+                    nc.sync.dma_start(out=g_sb[:, :, j, :], in_=g_rows[:, j, :].rearrange("p (k h) -> p k h", h=H_CHUNK))
 
+            if r % 2 == 1 and 3 <= r <= CHUNKS + 1:
+                factor(r - 3)
+            if yk is not None:
+                weigh_mean(yk, 0, FIRST)
+                join(yk, 0, FIRST, nc.gpsimd)
+                weigh_mean(yk, FIRST, ROWS)
+                join(yk, FIRST, ROWS, nc.gpsimd)
+            if r % 2 == 1 and 3 <= r <= CHUNKS + 1:
+                factor(r - 2)
+            share = SHIFT_ON_GPSIMD if r >= 4 else 0
             if new is not None:
                 maximum(new)
-            if old is not None:
-                mean(old)
-                turn_back(old)
+                shift(new, nc.gpsimd, ROWS - share, ROWS)
+            if wk is not None and wk != CHUNKS - 1:
+                write_ds(wk)
+            if mk is not None and r > 3:
+                mean(mk)
+                turn_back(mk)
+
+            if new is not None and r > 4:
+                shift(new, nc.vector, 0, ROWS - share)
             if mid is not None:
                 weigh_silu(mid)
-            if new is not None:
-                shift(new)
-            LAST = H // H_TILE - 1
-            if second_half is not None and second_half != LAST:
-                quantise_ds(second_half, 1)
-                products(second_half, 1)
-            if first_half is not None:
-                quantise_ds(first_half, 0)
-                products(first_half, 0)
-                if first_half == LAST:
-                    quantise_ds(first_half, 1)
+            if new is not None and r <= 4:
+                shift(new, nc.vector, 0, ROWS - share)
+            if mk is not None and r == 3:
+                mean(mk)
+                turn_back(mk)
+            todo, pend = pend, []
+            if wk is not None and wk % 2 == 1 and wk != CHUNKS - 1:
+                todo.append((wk // 2, 0, 4))
+                (todo if r > CHUNKS else pend).append((wk // 2, 4, 8))
+            for tile_no, w0, w1 in todo:
+                quantise_ds(tile_no, w0, w1)
             if mid is not None:
-                add_windows(mid, 0)
-                add_windows(mid, 1)
+                add_y(mid)
                 weigh_tanh(mid)
             for w in late:
                 quantise_x(w)
@@ -309,35 +340,30 @@ def tile_dendriticlayersilu_ffn_v_kernel(tc, x, template_flat, s, grad_out, out)
                     quantise_x(w - 1)
             if mine:
                 quantise_x(mine[-1])
-            long_window = dk is not None and r + 1 < CHUNKS
-            if old is not None:
-                weigh_mean(old, 0)
-                join(old, 0, nc.gpsimd)
-                weigh_mean(old, 1)
-                if long_window:
-                    join(old, 1, nc.gpsimd)
-            if dk is not None:
-                write_ds(dk)
-                if dk % CHUNKS_PER_TILE == CHUNKS_PER_TILE - 1:
-                    ds_ready = dk // CHUNKS_PER_TILE
-            if old is not None and not long_window:
-                join(old, 1, nc.vector)
 
-            if turn is not None:
-                guess_reciprocal(turn)
-                factor(turn)
+            if r == 0:
+                silu(0)
+                silu(1)
+            if new is not None and r % 2 == 0 and r > 0:
+                silu(new)
+                silu(new + 1)
+            if r % 2 == 0 and 2 <= r <= CHUNKS:
+                guess_reciprocals(r - 2)
             if new is not None:
                 tanh(new)
                 exponential(new)
             if r == 0:
                 turn_grad_out()
+            for tile_no, w0, w1 in todo:
+                products(tile_no, w0, w1)
+                empty_and_store(tile_no, w0, w1, [nc.scalar.copy])
+            if new is not None:
+                add_z(new)
             for w in late:
                 regroup_x(w, nc.scalar.copy)
-            if second_half is not None and second_half != LAST:
-                empty_and_store(second_half, 1, [nc.scalar.copy])
-            if first_half is not None and first_half != LAST:
-                empty_and_store(first_half, 0, [nc.scalar.copy])
-            if first_half == LAST:
-                empty_and_store(LAST, 0, [nc.scalar.copy, nc.vector.tensor_copy])
-                products(LAST, 1)
-                empty_and_store(LAST, 1, [nc.scalar.copy, nc.vector.tensor_copy])
+            if wk == CHUNKS - 1:
+                for w0, w1 in ((0, 4), (4, 8)):
+                    write_ds(wk, ((w0, w1),))
+                    quantise_ds(LAST, w0, w1)
+                    products(LAST, w0, w1, True)
+                    empty_and_store(LAST, w0, w1, [nc.scalar.copy] if w0 == 0 else [nc.vector.tensor_copy, nc.scalar.copy], True)

@@ -33,7 +33,7 @@ X_ON_SCALAR = (5,6,7)
 X_PER_ROUND = 3
 
 FIRST = 80
-SHIFT_ON_GPSIMD = 0
+SHIFT_ON_GPSIMD = 64
 FLOPS = 2 * TOKENS * H * W * K
 BYTES = TOKENS * W * K * 2 + TOKENS * H * W * 4 + TOKENS * H * 2 + H * W * K * 4
 
@@ -227,17 +227,20 @@ def tile_dendriticlayersilu_ffn_v_kernel(tc, x, template_flat, s, grad_out, out)
             )
 
         def regroup_x(w, copier):
-            x_grouped[w] = three.tile([P, K, PACK], BF16, align_bytes=64, name="x_grouped")
+            pair, half = divmod(w, 2)
+            if half == 0:
+                x_grouped[pair] = two.tile([P, 2, K, PACK], BF16, align_bytes=64, name="x_grouped")
             copier(
-                out=x_grouped[w][:].rearrange("p (c i) j -> p c j i", i=4),
+                out=x_grouped[pair][:, half, :, :].rearrange("p (c i) j -> p c j i", i=4),
                 in_=x_raw[w][:].rearrange("p j (c i) -> p c j i", i=4),
             )
 
-        def quantise_x(w):
+        def quantise_x(pair):
+            ws = slice(2 * pair, 2 * pair + 2)
             nc.vector.quantize_mx(
-                out=x_codes[:, w, :].bitcast(E4M3_X4),
-                scales=x_scales[:, w, :],
-                in_=x_grouped[w][:].rearrange("p c j -> p (c j)"),
+                out=x_codes[:, ws, :].rearrange("p w c -> p (w c)").bitcast(E4M3_X4),
+                scales=x_scales[:, ws, :].rearrange("p w c -> p (w c)"),
+                in_=x_grouped[pair][:].rearrange("p w c j -> p (w c j)"),
             )
 
         accs = {}
@@ -302,7 +305,7 @@ def tile_dendriticlayersilu_ffn_v_kernel(tc, x, template_flat, s, grad_out, out)
                 join(yk, FIRST, ROWS, nc.gpsimd)
             if r % 2 == 1 and 3 <= r <= CHUNKS + 1:
                 factor(r - 2)
-            share = SHIFT_ON_GPSIMD if r >= 4 else 0
+            share = SHIFT_ON_GPSIMD if r >= 5 else 0
             if new is not None:
                 maximum(new)
                 shift(new, nc.gpsimd, ROWS - share, ROWS)
@@ -323,23 +326,25 @@ def tile_dendriticlayersilu_ffn_v_kernel(tc, x, template_flat, s, grad_out, out)
                 turn_back(mk)
             todo, pend = pend, []
             if wk is not None and wk % 2 == 1 and wk != CHUNKS - 1:
+                quantise_ds(wk // 2, 0, W)
                 todo.append((wk // 2, 0, 4))
                 (todo if r > CHUNKS else pend).append((wk // 2, 4, 8))
-            for tile_no, w0, w1 in todo:
-                quantise_ds(tile_no, w0, w1)
             if mid is not None:
                 add_y(mid)
                 weigh_tanh(mid)
             for w in late:
-                quantise_x(w)
+                if w % 2 == 1:
+                    quantise_x(w // 2)
             late = [w for w in windows if w in X_ON_SCALAR]
             mine = [w for w in windows if w not in X_ON_SCALAR]
+            ready = None
             for w in mine:
                 regroup_x(w, nc.vector.tensor_copy)
-                if w - 1 in mine:
-                    quantise_x(w - 1)
-            if mine:
-                quantise_x(mine[-1])
+                if ready is not None:
+                    quantise_x(ready)
+                ready = w // 2 if w % 2 == 1 else None
+            if ready is not None:
+                quantise_x(ready)
 
             if r == 0:
                 silu(0)

@@ -1,3 +1,4 @@
+import math
 from contextlib import ExitStack
 
 import concourse.mybir as mybir
@@ -26,14 +27,18 @@ CHUNKS_PER_TILE = H_TILE // H_CHUNK
 ROWS = PACK * H_CHUNK
 BLOCKS = ROWS // P
 HALF_WINDOWS = 4
-ACC_BANKS = 3
+SHIFT_ON_TENSOR = 64
+TFROM = 4
+ACC_BANKS = 2
 STORE_BANKS = 2
-X_PLAN = ((0,1,2),(3,4),(),(5,),(),(6,7))
-X_ON_SCALAR = (5,6,7)
+X_PLAN = ((0,1),(2,),(),(3,),(),(4,5),(),(6,7))
+X_ON_SCALAR = (3,4,5,6,7)
 X_PER_ROUND = 3
 
 FIRST = 80
-SHIFT_ON_GPSIMD = 64
+SHIFT_ON_GPSIMD = 0
+LN2 = math.log(2.0)
+HALVES = ((0, 4), (4, 8))
 FLOPS = 2 * TOKENS * H * W * K
 BYTES = TOKENS * W * K * 2 + TOKENS * H * W * 4 + TOKENS * H * 2 + H * W * K * 4
 
@@ -53,7 +58,8 @@ def tile_dendriticlayersilu_ffn_v_kernel(tc, x, template_flat, s, grad_out, out)
         four = stack.enter_context(tc.tile_pool(name="four", bufs=4))
         three = stack.enter_context(tc.tile_pool(name="three", bufs=3))
         two = stack.enter_context(tc.tile_pool(name="two", bufs=2))
-        out_pool = stack.enter_context(tc.tile_pool(name="out_pool", bufs=4))
+        out_pool = stack.enter_context(tc.tile_pool(name="out_pool", bufs=5))
+        shift_psum = stack.enter_context(tc.psum_pool(name="shift_psum", bufs=1))
         z_psum = stack.enter_context(tc.psum_pool(name="z_psum", bufs=1))
         sums_psum = stack.enter_context(tc.psum_pool(name="sums_psum", bufs=2))
         acc_psum = stack.enter_context(tc.psum_pool(name="acc_psum", bufs=ACC_BANKS))
@@ -72,6 +78,7 @@ def tile_dendriticlayersilu_ffn_v_kernel(tc, x, template_flat, s, grad_out, out)
         nc.scalar.activation(out=warm[:], in_=warm[:], func=ACT.Silu)
 
         s_sb, top, e, m1, a1 = {}, {}, {}, {}, {}
+        shifted = {}
         z_t, sums_t, back, guess, yc_t = {}, {}, {}, {}, {}
         x_raw, x_grouped, ds_grouped, quantised, out_sb = {}, {}, {}, {}, {}
 
@@ -97,15 +104,18 @@ def tile_dendriticlayersilu_ffn_v_kernel(tc, x, template_flat, s, grad_out, out)
 
         def tanh(k):
             m1[k] = five.tile(wide, F32, name="m1")
-            nc.scalar.activation(out=m1[k][:], in_=s_sb[k][:], func=ACT.Tanh, scale=0.5)
+            nc.scalar.activation(out=m1[k][:], in_=s_sb[k][:], func=ACT.Tanh, scale=-0.5)
 
         def exponential(k):
-            nc.scalar.activation(out=e[k][:], in_=e[k][:], func=ACT.Exp)
+            r0 = ROWS - (SHIFT_ON_TENSOR if k >= TFROM else 0)
+            nc.scalar.activation(out=e[k][:, 0:r0, :], in_=e[k][:, 0:r0, :], func=ACT.Exp)
+            if r0 < ROWS:
+                nc.scalar.activation(out=e[k][:, r0:ROWS, :], in_=shifted[k][:, 0 : SHIFT_ON_TENSOR * W].rearrange("p (r w) -> p r w", w=W), func=ACT.Exp)
 
         def guess_reciprocals(k):
             pair = two.tile([P, 2 * ROWS], F32, name="guess")
             nc.scalar.activation(out=pair[:], in_=z_t[0][:], func=ACT.Ln)
-            nc.scalar.activation(out=pair[:], in_=pair[:], func=ACT.Exp, scale=-1.0)
+            nc.scalar.activation(out=pair[:], in_=pair[:], func=ACT.Exp, scale=-1.0, bias=-LN2)
             guess[k], guess[k + 1] = pair[:, 0:ROWS], pair[:, ROWS : 2 * ROWS]
 
         def add_windows(sums, terms):
@@ -144,14 +154,24 @@ def tile_dendriticlayersilu_ffn_v_kernel(tc, x, template_flat, s, grad_out, out)
                     rows = g_sb[:, k, :, :].rearrange("p j h -> p (j h)")
                     nc.tensor.transpose(out=g_ps[:, i, :], in_=rows[:, b * P : (b + 1) * P], identity=identity_bf[:])
                 n = CHUNKS * BLOCKS // 2
-                nc.scalar.mul(out=g_t[:, half * n : (half + 1) * n, :], in_=g_ps[:], mul=-0.5)
+                nc.scalar.copy(out=g_t[:, half * n : (half + 1) * n, :], in_=g_ps[:])
 
         def maximum(k):
             top[k] = two.tile([P, ROWS], F32, name="top")
             pieces = PACK if k == 0 else 1
             for i in range(pieces):
                 rows = slice(i * ROWS // pieces, (i + 1) * ROWS // pieces)
-                nc.vector.tensor_reduce(out=top[k][:, rows], in_=s_sb[k][:, rows, :], axis=AXIS.X, op=ALU.max)
+                nc.vector.tensor_reduce(out=top[k][:, rows], in_=s_sb[k][:, rows, :], axis=AXIS.X, op=ALU.max, negate=True)
+
+        def shift_on_tensor(k):
+            r0 = ROWS - SHIFT_ON_TENSOR
+            shifted[k] = shift_psum.tile([P, 2 * ROWS], F32, name="shifted")
+            cells = shifted[k][:, 0 : SHIFT_ON_TENSOR * W]
+            nc.tensor.matmul(out=cells, lhsT=identity[:], rhs=s_sb[k][:, r0:ROWS, :].rearrange("p r w -> p (r w)"), start=True, stop=False)
+            nc.tensor.matmul(
+                out=cells.rearrange("p (r w) -> p r w", w=W), lhsT=identity[:],
+                rhs=top[k][:, r0:ROWS].unsqueeze(2).to_broadcast([P, SHIFT_ON_TENSOR, W]), start=False, stop=True,
+            )
 
         def shift(k, engine, r0, r1):
             if k not in e:
@@ -159,7 +179,7 @@ def tile_dendriticlayersilu_ffn_v_kernel(tc, x, template_flat, s, grad_out, out)
             if r0 < r1:
                 engine.tensor_tensor(
                     out=e[k][:, r0:r1, :], in0=s_sb[k][:, r0:r1, :],
-                    in1=top[k][:, r0:r1].unsqueeze(2).to_broadcast([P, r1 - r0, W]), op=ALU.subtract,
+                    in1=top[k][:, r0:r1].unsqueeze(2).to_broadcast([P, r1 - r0, W]), op=ALU.add,
                 )
 
         def weigh_silu(k):
@@ -169,12 +189,12 @@ def tile_dendriticlayersilu_ffn_v_kernel(tc, x, template_flat, s, grad_out, out)
 
         def weigh_tanh(k):
             nc.vector.scalar_tensor_tensor(
-                out=m1[k][:], in0=m1[k][:], scalar=-3.0, in1=a1[k][:], op0=ALU.add, op1=ALU.mult
+                out=m1[k][:], in0=m1[k][:], scalar=3.0, in1=a1[k][:], op0=ALU.add, op1=ALU.mult
             )
 
         def mean(k):
             nc.vector.scalar_tensor_tensor(
-                out=yc_t[k][:, ROWS : 2 * ROWS], in0=sums_t[k][:, 0:ROWS], scalar=2.0, in1=guess[k],
+                out=yc_t[k][:, ROWS : 2 * ROWS], in0=sums_t[k][:, 0:ROWS], scalar=-4.0, in1=guess[k],
                 op0=ALU.mult, op1=ALU.mult,
             )
 
@@ -186,22 +206,21 @@ def tile_dendriticlayersilu_ffn_v_kernel(tc, x, template_flat, s, grad_out, out)
                 in1=guess[k], op=ALU.mult,
             )
 
-        def weigh_mean(k, r0, r1):
+        def weigh_mean(k, r0, r1, w0=0, w1=W):
             rows = slice(r0, r1)
             y2 = back[k][:, ROWS : 2 * ROWS]
             nc.vector.scalar_tensor_tensor(
-                out=e[k][:, rows, :], in0=y2[:, rows].unsqueeze(2).to_broadcast([P, r1 - r0, W]), scalar=-2.0,
-                in1=e[k][:, rows, :], op0=ALU.add, op1=ALU.mult,
+                out=e[k][:, rows, w0:w1], in0=y2[:, rows].unsqueeze(2).to_broadcast([P, r1 - r0, w1 - w0]), scalar=2.0,
+                in1=e[k][:, rows, w0:w1], op0=ALU.add, op1=ALU.mult,
             )
 
-        def join(k, r0, r1, engine):
+        def join(k, r0, r1, w0=0, w1=W):
             rows = slice(r0, r1)
-            if r0 < r1:
-                engine.tensor_tensor(out=m1[k][:, rows, :], in0=m1[k][:, rows, :], in1=e[k][:, rows, :], op=ALU.add)
+            nc.gpsimd.tensor_tensor(out=m1[k][:, rows, w0:w1], in0=m1[k][:, rows, w0:w1], in1=e[k][:, rows, w0:w1], op=ALU.add)
 
-        def write_ds(k, pieces=((0, 4), (4, 8))):
+        def write_ds(k, pieces=HALVES):
             tile_no = k // CHUNKS_PER_TILE
-            if k % CHUNKS_PER_TILE == 0:
+            if k % CHUNKS_PER_TILE == 0 and pieces[0][0] == 0:
                 ds_grouped[tile_no] = two.tile([P, W, H_TILE, PACK], BF16, align_bytes=64, name="ds_grouped")
             f0 = (k % CHUNKS_PER_TILE) * H_CHUNK
             m1_v = m1[k][:].rearrange("p (j h) w -> p h j w", j=PACK)
@@ -247,7 +266,7 @@ def tile_dendriticlayersilu_ffn_v_kernel(tc, x, template_flat, s, grad_out, out)
 
         def products(tile_no, w0, w1, spare=False):
             ds_codes, ds_scales = quantised[tile_no]
-            all_banks = [(acc_psum, "acc")] * ACC_BANKS + [(z_psum, "z_t")] + [(sums_psum, "sums_t")] * 2 + [(sums_psum, "back")] * 2
+            all_banks = [(acc_psum, "acc")] * ACC_BANKS + [(shift_psum, "shifted"), (z_psum, "z_t")] + [(sums_psum, "sums_t")] * 2 + [(sums_psum, "back")] * 2
             for w in range(w0, w1):
                 pool, tag = all_banks[w] if spare else (acc_psum, "acc")
                 accs[w] = pool.tile([H_TILE, K], F32, name=tag)
@@ -277,7 +296,7 @@ def tile_dendriticlayersilu_ffn_v_kernel(tc, x, template_flat, s, grad_out, out)
         late = []
         pend = []
         LAST = H // H_TILE - 1
-        for r in range(CHUNKS + 6):
+        for r in range(CHUNKS + 4):
             def stage(lag):
                 return r - lag if 0 <= r - lag < CHUNKS else None
 
@@ -296,36 +315,43 @@ def tile_dendriticlayersilu_ffn_v_kernel(tc, x, template_flat, s, grad_out, out)
                 for j in range(PACK):
                     nc.sync.dma_start(out=g_sb[:, :, j, :], in_=g_rows[:, j, :].rearrange("p (k h) -> p k h", h=H_CHUNK))
 
-            if r % 2 == 1 and 3 <= r <= CHUNKS + 1:
+            pair_due = r % 2 == 1 and 3 <= r <= CHUNKS + 1
+            if pair_due and yk is None:
                 factor(r - 3)
-            if yk is not None:
+            if yk is not None and yk != CHUNKS - 1:
                 weigh_mean(yk, 0, FIRST)
-                join(yk, 0, FIRST, nc.gpsimd)
+                join(yk, 0, FIRST)
+                if pair_due:
+                    factor(r - 3)
                 weigh_mean(yk, FIRST, ROWS)
-                join(yk, FIRST, ROWS, nc.gpsimd)
-            if r % 2 == 1 and 3 <= r <= CHUNKS + 1:
+                join(yk, FIRST, ROWS)
+            if pair_due:
                 factor(r - 2)
             share = SHIFT_ON_GPSIMD if r >= 5 else 0
             if new is not None:
                 maximum(new)
-                shift(new, nc.gpsimd, ROWS - share, ROWS)
-            if wk is not None and wk != CHUNKS - 1:
+                tens = SHIFT_ON_TENSOR if new >= TFROM else 0
+                if tens:
+                    shift_on_tensor(new)
+                shift(new, nc.gpsimd, ROWS - tens - share, ROWS - tens)
+            if wk is not None and wk < CHUNKS - 2:
                 write_ds(wk)
             if mk is not None and r > 3:
                 mean(mk)
                 turn_back(mk)
 
-            if new is not None and r > 4:
-                shift(new, nc.vector, 0, ROWS - share)
+            shift_first = r > 4 or r % 2 == 1
+            if new is not None and shift_first:
+                shift(new, nc.vector, 0, ROWS - tens - share)
             if mid is not None:
                 weigh_silu(mid)
-            if new is not None and r <= 4:
-                shift(new, nc.vector, 0, ROWS - share)
+            if new is not None and not shift_first:
+                shift(new, nc.vector, 0, ROWS - tens - share)
             if mk is not None and r == 3:
                 mean(mk)
                 turn_back(mk)
-            todo, pend = pend, []
-            if wk is not None and wk % 2 == 1 and wk != CHUNKS - 1:
+            todo, pend = (pend, []) if r != 7 else ([], pend)
+            if wk is not None and wk % 2 == 1:
                 quantise_ds(wk // 2, 0, W)
                 todo.append((wk // 2, 0, 4))
                 (todo if r > CHUNKS else pend).append((wk // 2, 4, 8))
@@ -366,9 +392,16 @@ def tile_dendriticlayersilu_ffn_v_kernel(tc, x, template_flat, s, grad_out, out)
                 add_z(new)
             for w in late:
                 regroup_x(w, nc.scalar.copy)
-            if wk == CHUNKS - 1:
-                for w0, w1 in ((0, 4), (4, 8)):
-                    write_ds(wk, ((w0, w1),))
+            if yk == CHUNKS - 1:
+                for w0, w1 in HALVES:
+                    weigh_mean(yk, 0, ROWS, w0, w1)
+                    join(yk, 0, ROWS, w0, w1)
+                write_ds(yk - 1, HALVES[:1])
+                write_ds(yk, HALVES[:1])
+                write_ds(yk - 1, HALVES[1:])
+                for w0, w1 in HALVES:
+                    if w0 > 0:
+                        write_ds(yk, HALVES[1:])
                     quantise_ds(LAST, w0, w1)
                     products(LAST, w0, w1, True)
                     empty_and_store(LAST, w0, w1, [nc.scalar.copy] if w0 == 0 else [nc.vector.tensor_copy, nc.scalar.copy], True)

@@ -246,20 +246,17 @@ def tile_dendriticlayersilu_ffn_v_kernel(tc, x, template_flat, s, grad_out, out)
             )
 
         def regroup_x(w, copier):
-            pair, half = divmod(w, 2)
-            if half == 0:
-                x_grouped[pair] = two.tile([P, 2, K, PACK], BF16, align_bytes=64, name="x_grouped")
+            x_grouped[w] = three.tile([P, K, PACK], BF16, align_bytes=64, name="x_grouped")
             copier(
-                out=x_grouped[pair][:, half, :, :].rearrange("p (c i) j -> p c j i", i=4),
+                out=x_grouped[w][:].rearrange("p (c i) j -> p c j i", i=4),
                 in_=x_raw[w][:].rearrange("p j (c i) -> p c j i", i=4),
             )
 
-        def quantise_x(pair):
-            ws = slice(2 * pair, 2 * pair + 2)
+        def quantise_x(w):
             nc.vector.quantize_mx(
-                out=x_codes[:, ws, :].rearrange("p w c -> p (w c)").bitcast(E4M3_X4),
-                scales=x_scales[:, ws, :].rearrange("p w c -> p (w c)"),
-                in_=x_grouped[pair][:].rearrange("p w c j -> p (w c j)"),
+                out=x_codes[:, w, :].bitcast(E4M3_X4),
+                scales=x_scales[:, w, :],
+                in_=x_grouped[w][:].rearrange("p c j -> p (c j)"),
             )
 
         accs = {}
@@ -352,15 +349,15 @@ def tile_dendriticlayersilu_ffn_v_kernel(tc, x, template_flat, s, grad_out, out)
                 turn_back(mk)
             todo, pend = (pend, []) if r != 7 else ([], pend)
             if wk is not None and wk % 2 == 1:
-                quantise_ds(wk // 2, 0, W)
                 todo.append((wk // 2, 0, 4))
                 (todo if r > CHUNKS else pend).append((wk // 2, 4, 8))
+            for tile_no, w0, w1 in todo:
+                quantise_ds(tile_no, w0, w1)
             if mid is not None:
                 add_y(mid)
                 weigh_tanh(mid)
             for w in late:
-                if w % 2 == 1:
-                    quantise_x(w // 2)
+                quantise_x(w)
             late = [w for w in windows if w in X_ON_SCALAR]
             mine = [w for w in windows if w not in X_ON_SCALAR]
             ready = None
@@ -368,7 +365,7 @@ def tile_dendriticlayersilu_ffn_v_kernel(tc, x, template_flat, s, grad_out, out)
                 regroup_x(w, nc.vector.tensor_copy)
                 if ready is not None:
                     quantise_x(ready)
-                ready = w // 2 if w % 2 == 1 else None
+                ready = w
             if ready is not None:
                 quantise_x(ready)
 

@@ -31,7 +31,7 @@ SHIFT_ON_TENSOR = 64
 TFROM = 4
 ACC_BANKS = 2
 STORE_BANKS = 2
-X_PLAN = ((0,1),(2,),(),(3,),(),(4,5),(),(6,7))
+X_PLAN = ((0,1),(2,),(),(3,),(),(4,),(5,),(6,7))
 X_ON_SCALAR = (3,4,5,6,7)
 X_PER_ROUND = 3
 
@@ -337,7 +337,7 @@ def tile_dendriticlayersilu_ffn_v_kernel(tc, x, template_flat, s, grad_out, out)
                 mean(mk)
                 turn_back(mk)
 
-            shift_first = r > 4 or r % 2 == 1
+            shift_first = r in (1, 3)
             if new is not None and shift_first:
                 shift(new, nc.vector, 0, ROWS - tens - share)
             if mid is not None:
@@ -355,7 +355,6 @@ def tile_dendriticlayersilu_ffn_v_kernel(tc, x, template_flat, s, grad_out, out)
                 quantise_ds(tile_no, w0, w1)
             if mid is not None:
                 add_y(mid)
-                weigh_tanh(mid)
             for w in late:
                 quantise_x(w)
             late = [w for w in windows if w in X_ON_SCALAR]
@@ -368,7 +367,8 @@ def tile_dendriticlayersilu_ffn_v_kernel(tc, x, template_flat, s, grad_out, out)
                 ready = w
             if ready is not None:
                 quantise_x(ready)
-
+            if mid is not None:
+                weigh_tanh(mid)
             if r == 0:
                 silu(0)
                 silu(1)

@@ -31,8 +31,8 @@ SHIFT_ON_TENSOR = 64
 TFROM = 4
 ACC_BANKS = 2
 STORE_BANKS = 2
-X_PLAN = ((0,1),(2,),(),(3,),(),(4,),(5,),(6,7))
-X_ON_SCALAR = (3,4,5,6,7)
+X_PLAN = ((0,1),(),(),(2,),(3,),(4,),(5,),(6,7))
+X_ON_SCALAR = (2,3,4,5,6,7)
 X_PER_ROUND = 3
 
 FIRST = 80
@@ -261,11 +261,10 @@ def tile_dendriticlayersilu_ffn_v_kernel(tc, x, template_flat, s, grad_out, out)
 
         accs = {}
 
-        def products(tile_no, w0, w1, spare=False):
+        def products(tile_no, w0, w1, banks):
             ds_codes, ds_scales = quantised[tile_no]
-            all_banks = [(acc_psum, "acc")] * ACC_BANKS + [(shift_psum, "shifted"), (z_psum, "z_t")] + [(sums_psum, "sums_t")] * 2 + [(sums_psum, "back")] * 2
             for w in range(w0, w1):
-                pool, tag = all_banks[w] if spare else (acc_psum, "acc")
+                pool, tag = banks[w % len(banks)]
                 accs[w] = pool.tile([H_TILE, K], F32, name=tag)
                 nc.tensor.matmul_mx(
                     out=accs[w][:],
@@ -292,6 +291,7 @@ def tile_dendriticlayersilu_ffn_v_kernel(tc, x, template_flat, s, grad_out, out)
 
         late = []
         pend = []
+        banks = [(acc_psum, "acc")] * ACC_BANKS
         LAST = H // H_TILE - 1
         for r in range(CHUNKS + 4):
             def stage(lag):
@@ -311,6 +311,11 @@ def tile_dendriticlayersilu_ffn_v_kernel(tc, x, template_flat, s, grad_out, out)
             if r == 0:
                 for j in range(PACK):
                     nc.sync.dma_start(out=g_sb[:, :, j, :], in_=g_rows[:, j, :].rearrange("p (k h) -> p k h", h=H_CHUNK))
+
+            if r % 2 == 0 and r < CHUNKS:
+                if mid is not None:
+                    silu(mid)
+                silu(new)
 
             pair_due = r % 2 == 1 and 3 <= r <= CHUNKS + 1
             if pair_due and yk is None:
@@ -347,48 +352,50 @@ def tile_dendriticlayersilu_ffn_v_kernel(tc, x, template_flat, s, grad_out, out)
             if mk is not None and r == 3:
                 mean(mk)
                 turn_back(mk)
+            if r == CHUNKS:
+                banks.append((shift_psum, "shifted"))
+            if r == CHUNKS + 1:
+                banks.append((z_psum, "z_t"))
+            if yk == CHUNKS - 1:
+                banks += [(sums_psum, "sums_t")] * 2 + [(sums_psum, "back")] * 2
             todo, pend = (pend, []) if r != 7 else ([], pend)
             if wk is not None and wk % 2 == 1:
                 todo.append((wk // 2, 0, 4))
                 (todo if r > CHUNKS else pend).append((wk // 2, 4, 8))
-            for tile_no, w0, w1 in todo:
-                quantise_ds(tile_no, w0, w1)
-            if mid is not None:
+            if wk is not None and wk % 2 == 1:
+                quantise_ds(wk // 2, 0, W)
+            if mid is not None and not (r == 1):
                 add_y(mid)
             for w in late:
                 quantise_x(w)
-            late = [w for w in windows if w in X_ON_SCALAR]
-            mine = [w for w in windows if w not in X_ON_SCALAR]
-            ready = None
-            for w in mine:
-                regroup_x(w, nc.vector.tensor_copy)
-                if ready is not None:
-                    quantise_x(ready)
-                ready = w
-            if ready is not None:
-                quantise_x(ready)
+            late = list(windows)
+            for w in windows:
+                if w not in X_ON_SCALAR:
+                    regroup_x(w, nc.vector.tensor_copy)
+            if r == 0:
+                quantise_x(late.pop(0))
             if mid is not None:
                 weigh_tanh(mid)
-            if r == 0:
-                silu(0)
-                silu(1)
-            if new is not None and r % 2 == 0 and r > 0:
-                silu(new)
-                silu(new + 1)
             if r % 2 == 0 and 2 <= r <= CHUNKS:
                 guess_reciprocals(r - 2)
             if new is not None:
                 tanh(new)
                 exponential(new)
+                if new == CHUNKS - 1:
+                    silu(new)
             if r == 0:
                 turn_grad_out()
-            for tile_no, w0, w1 in todo:
-                products(tile_no, w0, w1)
-                empty_and_store(tile_no, w0, w1, [nc.scalar.copy])
-            if new is not None:
+            if r == 1:
                 add_z(new)
-            for w in late:
-                regroup_x(w, nc.scalar.copy)
+                add_y(mid)
+            for tile_no, w0, w1 in todo:
+                products(tile_no, w0, w1, banks)
+                empty_and_store(tile_no, w0, w1, [nc.scalar.copy])
+            if new is not None and not (r == 1):
+                add_z(new)
+            for w in windows:
+                if w in X_ON_SCALAR:
+                    regroup_x(w, nc.scalar.copy)
             if yk == CHUNKS - 1:
                 for w0, w1 in HALVES:
                     weigh_mean(yk, 0, ROWS, w0, w1)
@@ -400,5 +407,5 @@ def tile_dendriticlayersilu_ffn_v_kernel(tc, x, template_flat, s, grad_out, out)
                     if w0 > 0:
                         write_ds(yk, HALVES[1:])
                     quantise_ds(LAST, w0, w1)
-                    products(LAST, w0, w1, True)
+                    products(LAST, w0, w1, banks)
                     empty_and_store(LAST, w0, w1, [nc.scalar.copy] if w0 == 0 else [nc.vector.tensor_copy, nc.scalar.copy], True)

@@ -248,8 +248,8 @@ def tile_dendriticlayersilu_ffn_v_kernel(tc, x, template_flat, s, grad_out, out)
         def regroup_x(w, copier):
             x_grouped[w] = three.tile([P, K, PACK], BF16, align_bytes=64, name="x_grouped")
             copier(
-                out=x_grouped[w][:].rearrange("p (c i) j -> p c j i", i=4),
-                in_=x_raw[w][:].rearrange("p j (c i) -> p c j i", i=4),
+                out=x_grouped[w][:].rearrange("p (c i) j -> p c j i", i=8),
+                in_=x_raw[w][:].rearrange("p j (c i) -> p c j i", i=8),
             )
 
         def quantise_x(w):

@@ -27,6 +27,8 @@ CHUNKS_PER_TILE = H_TILE // H_CHUNK
 ROWS = PACK * H_CHUNK
 BLOCKS = ROWS // P
 HALF_WINDOWS = 4
+JOIN_ON_TENSOR = (6,)
+JOIN_FEATURES = 16
 SHIFT_ON_TENSOR = 64
 TFROM = 4
 ACC_BANKS = 2
@@ -78,7 +80,8 @@ def tile_dendriticlayersilu_ffn_v_kernel(tc, x, template_flat, s, grad_out, out)
         nc.scalar.activation(out=warm[:], in_=warm[:], func=ACT.Silu)
 
         s_sb, top, e, m1, a1 = {}, {}, {}, {}, {}
-        shifted = {}
+        shifted, joined, c_sb = {}, {}, {}
+        H_SPLIT = H_CHUNK - JOIN_FEATURES
         z_t, sums_t, back, guess, yc_t = {}, {}, {}, {}, {}
         x_raw, x_grouped, ds_grouped, quantised, out_sb = {}, {}, {}, {}, {}
 
@@ -218,17 +221,44 @@ def tile_dendriticlayersilu_ffn_v_kernel(tc, x, template_flat, s, grad_out, out)
             rows = slice(r0, r1)
             nc.gpsimd.tensor_tensor(out=m1[k][:, rows, w0:w1], in0=m1[k][:, rows, w0:w1], in1=e[k][:, rows, w0:w1], op=ALU.add)
 
+        def join_on_tensor(k):
+            joined[k] = z_psum.tile([P, 2 * ROWS], F32, name="z_t")
+            cells = joined[k][:].rearrange("p (j x) -> p j x", j=PACK)
+            for i, term in enumerate((m1[k], e[k])):
+                part = term[:].rearrange("p (j h) w -> p j (h w)", j=PACK)[:, :, H_SPLIT * W :]
+                nc.tensor.matmul(out=cells, lhsT=identity[:], rhs=part, start=(i == 0), stop=(i == 1))
+
+        def keep_factor(k):
+            c_sb[k] = two.tile([P, PACK, JOIN_FEATURES], F32, name="c_sb")
+            nc.scalar.copy(out=c_sb[k][:], in_=back[k][:, 0:ROWS].rearrange("p (j h) -> p j h", j=PACK)[:, :, H_SPLIT:])
+
+        def join_first_features(k, j0, j1):
+            part = slice(0, H_SPLIT * W)
+            m1_v = m1[k][:].rearrange("p (j h) w -> p j (h w)", j=PACK)[:, j0:j1, part]
+            e_v = e[k][:].rearrange("p (j h) w -> p j (h w)", j=PACK)[:, j0:j1, part]
+            nc.gpsimd.tensor_tensor(out=m1_v, in0=m1_v, in1=e_v, op=ALU.add)
+
         def write_ds(k, pieces=HALVES):
             tile_no = k // CHUNKS_PER_TILE
             if k % CHUNKS_PER_TILE == 0 and pieces[0][0] == 0:
                 ds_grouped[tile_no] = two.tile([P, W, H_TILE, PACK], BF16, align_bytes=64, name="ds_grouped")
             f0 = (k % CHUNKS_PER_TILE) * H_CHUNK
             m1_v = m1[k][:].rearrange("p (j h) w -> p h j w", j=PACK)
+            h1 = H_SPLIT if k in JOIN_ON_TENSOR else H_CHUNK
+            if k in JOIN_ON_TENSOR:
+                j_v = joined[k][:].rearrange("p (j h w) -> p h j w", j=PACK, w=W)
+                for w0, w1 in pieces:
+                    nc.vector.tensor_tensor(
+                        out=ds_grouped[tile_no][:, w0:w1, f0 + h1 : f0 + H_CHUNK, :].rearrange("p w h j -> p h j w"),
+                        in0=j_v[:, :, :, w0:w1],
+                        in1=c_sb[k][:].rearrange("p j h -> p h j").unsqueeze(3).to_broadcast([P, JOIN_FEATURES, PACK, w1 - w0]),
+                        op=ALU.mult,
+                    )
             for w0, w1 in pieces:
-                c_v = back[k][:, 0:ROWS].rearrange("p (j h) -> p h j", j=PACK).unsqueeze(3).to_broadcast([P, H_CHUNK, PACK, w1 - w0])
+                c_v = back[k][:, 0:ROWS].rearrange("p (j h) -> p h j", j=PACK)[:, 0:h1].unsqueeze(3).to_broadcast([P, h1, PACK, w1 - w0])
                 nc.vector.tensor_tensor(
-                    out=ds_grouped[tile_no][:, w0:w1, f0 : f0 + H_CHUNK, :].rearrange("p w h j -> p h j w"),
-                    in0=m1_v[:, :, :, w0:w1],
+                    out=ds_grouped[tile_no][:, w0:w1, f0 : f0 + h1, :].rearrange("p w h j -> p h j w"),
+                    in0=m1_v[:, 0:h1, :, w0:w1],
                     in1=c_v,
                     op=ALU.mult,
                 )
@@ -320,7 +350,16 @@ def tile_dendriticlayersilu_ffn_v_kernel(tc, x, template_flat, s, grad_out, out)
             pair_due = r % 2 == 1 and 3 <= r <= CHUNKS + 1
             if pair_due and yk is None:
                 factor(r - 3)
-            if yk is not None and yk != CHUNKS - 1:
+            if yk in JOIN_ON_TENSOR:
+                weigh_mean(yk, 0, H_CHUNK)
+                join_first_features(yk, 0, 1)
+                if pair_due:
+                    factor(r - 3)
+                weigh_mean(yk, H_CHUNK, ROWS)
+                keep_factor(yk)
+                join_on_tensor(yk)
+                join_first_features(yk, 1, PACK)
+            elif yk is not None and yk != CHUNKS - 1:
                 weigh_mean(yk, 0, FIRST)
                 join(yk, 0, FIRST)
                 if pair_due:
@@ -354,10 +393,8 @@ def tile_dendriticlayersilu_ffn_v_kernel(tc, x, template_flat, s, grad_out, out)
                 turn_back(mk)
             if r == CHUNKS:
                 banks.append((shift_psum, "shifted"))
-            if r == CHUNKS + 1:
-                banks.append((z_psum, "z_t"))
             if yk == CHUNKS - 1:
-                banks += [(sums_psum, "sums_t")] * 2 + [(sums_psum, "back")] * 2
+                banks += [(z_psum, "z_t")] + [(sums_psum, "sums_t")] * 2 + [(sums_psum, "back")] * 2
             todo, pend = (pend, []) if r != 7 else ([], pend)
             if wk is not None and wk % 2 == 1:
                 todo.append((wk // 2, 0, 4))

import math
from contextlib import ExitStack

import concourse.mybir as mybir
from concourse.masks import make_identity

F32 = mybir.dt.float32
BF16 = mybir.dt.bfloat16
U32 = mybir.dt.uint32
U8 = mybir.dt.uint8
E4M3_X4 = mybir.dt.float8_e4m3fn_x4
E5M2_X4 = mybir.dt.float8_e5m2_x4
ALU = mybir.AluOpType
ACT = mybir.ActivationFunctionType
AXIS = mybir.AxisListType

P = 128
PACK = 4
TOKENS = P * PACK
H = 512
W = 8
K = 512
H_TILE = 128
H_CHUNK = 64
CHUNKS = H // H_CHUNK
CHUNKS_PER_TILE = H_TILE // H_CHUNK
ROWS = PACK * H_CHUNK
BLOCKS = ROWS // P
HALF_WINDOWS = 4
JOIN_ON_TENSOR = (6,)
JOIN_FEATURES = 16
SHIFT_ON_TENSOR = 64
TFROM = 4
ACC_BANKS = 2
STORE_BANKS = 2
X_PLAN = ((0,1),(),(),(2,),(3,),(4,),(5,),(6,7))
X_ON_SCALAR = (2,3,4,5,6,7)
X_PER_ROUND = 3

FIRST = 80
SHIFT_ON_GPSIMD = 0
LN2 = math.log(2.0)
HALVES = ((0, 4), (4, 8))
FLOPS = 2 * TOKENS * H * W * K
BYTES = TOKENS * W * K * 2 + TOKENS * H * W * 4 + TOKENS * H * 2 + H * W * K * 4


def tile_dendriticlayersilu_ffn_v_kernel(tc, x, template_flat, s, grad_out, out):
    nc = tc.nc
    x_rows = x.rearrange("(p j) c -> p j c", j=PACK)
    s_rows = s.rearrange("(p j) h w -> p j h w", j=PACK)
    g_rows = grad_out.rearrange("(p j) h -> p j h", j=PACK)
    wide = [P, ROWS, W]

    with ExitStack() as stack:
        stack.enter_context(tc.manual_schedule())
        keep = stack.enter_context(tc.tile_pool(name="keep", bufs=1))
        x_raw_pool = stack.enter_context(tc.tile_pool(name="x_raw", bufs=3))
        five = stack.enter_context(tc.tile_pool(name="five", bufs=5))
        four = stack.enter_context(tc.tile_pool(name="four", bufs=4))
        three = stack.enter_context(tc.tile_pool(name="three", bufs=3))
        two = stack.enter_context(tc.tile_pool(name="two", bufs=2))
        out_pool = stack.enter_context(tc.tile_pool(name="out_pool", bufs=5))
        shift_psum = stack.enter_context(tc.psum_pool(name="shift_psum", bufs=1))
        z_psum = stack.enter_context(tc.psum_pool(name="z_psum", bufs=1))
        sums_psum = stack.enter_context(tc.psum_pool(name="sums_psum", bufs=2))
        acc_psum = stack.enter_context(tc.psum_pool(name="acc_psum", bufs=ACC_BANKS))

        identity = keep.tile([P, P], F32)
        make_identity(nc, identity[:])
        identity_bf = keep.tile([P, P], BF16)
        make_identity(nc, identity_bf[:])
        g_sb = keep.tile([P, CHUNKS, PACK, H_CHUNK], BF16)
        g_t = keep.tile([P, CHUNKS * BLOCKS, P], BF16)
        x_codes = keep.tile([P, W, K], U32, align_bytes=64)
        x_scales = keep.tile([P, W, K], U8, align_bytes=64)

        warm = keep.tile([P, 1], F32)
        nc.gpsimd.memset(warm[:], 0.0)
        nc.scalar.activation(out=warm[:], in_=warm[:], func=ACT.Silu)

        s_sb, top, e, m1, a1 = {}, {}, {}, {}, {}
        shifted, joined, c_sb = {}, {}, {}
        H_SPLIT = H_CHUNK - JOIN_FEATURES
        z_t, sums_t, back, guess, yc_t = {}, {}, {}, {}, {}
        x_raw, x_grouped, ds_grouped, quantised, out_sb = {}, {}, {}, {}, {}

        def spread(small):
            return small.unsqueeze(2).to_broadcast(wide)

        def load_s(k):
            s_sb[k] = three.tile([P, ROWS, W], F32, name="s_sb")
            features = slice(k * H_CHUNK, (k + 1) * H_CHUNK)
            if k == 0:
                for j in range(PACK):
                    nc.sync.dma_start(out=s_sb[k][:, j * H_CHUNK : (j + 1) * H_CHUNK, :], in_=s_rows[:, j, features, :])
            else:
                nc.sync.dma_start(out=s_sb[k][:].rearrange("p (j h) w -> p j h w", j=PACK), in_=s_rows[:, :, features, :])

        def load_x(w):
            x_raw[w] = x_raw_pool.tile([P, PACK, K], BF16, name="x_raw")
            nc.sync.dma_start(out=x_raw[w][:], in_=x_rows[:, :, w * K : (w + 1) * K])

        def silu(k):
            a1[k] = three.tile(wide, F32, name="a1")
            nc.scalar.activation(out=a1[k][:], in_=s_sb[k][:], func=ACT.Silu)

        def tanh(k):
            m1[k] = five.tile(wide, F32, name="m1")
            nc.scalar.activation(out=m1[k][:], in_=s_sb[k][:], func=ACT.Tanh, scale=-0.5)

        def exponential(k):
            r0 = ROWS - (SHIFT_ON_TENSOR if k >= TFROM else 0)
            nc.scalar.activation(out=e[k][:, 0:r0, :], in_=e[k][:, 0:r0, :], func=ACT.Exp)
            if r0 < ROWS:
                nc.scalar.activation(out=e[k][:, r0:ROWS, :], in_=shifted[k][:, 0 : SHIFT_ON_TENSOR * W].rearrange("p (r w) -> p r w", w=W), func=ACT.Exp)

        def guess_reciprocals(k):
            pair = two.tile([P, 2 * ROWS], F32, name="guess")
            nc.scalar.activation(out=pair[:], in_=z_t[0][:], func=ACT.Ln)
            nc.scalar.activation(out=pair[:], in_=pair[:], func=ACT.Exp, scale=-1.0, bias=-LN2)
            guess[k], guess[k + 1] = pair[:, 0:ROWS], pair[:, ROWS : 2 * ROWS]

        def add_windows(sums, terms):
            for b in range(BLOCKS):
                for w in range(W):
                    nc.tensor.matmul(
                        out=sums[:, b * P : (b + 1) * P],
                        lhsT=terms[:, b * P : (b + 1) * P, w],
                        rhs=identity[:],
                        is_transpose=True,
                        start=(w == 0),
                        stop=(w == W - 1),
                    )

        def add_z(k):
            if k % 2 == 0:
                z_t[0] = z_psum.tile([P, 2 * ROWS], F32, name="z_t")
            half = (k % 2) * ROWS
            add_windows(z_t[0][:, half : half + ROWS], e[k])

        def add_y(k):
            sums_t[k] = sums_psum.tile([P, 2 * ROWS], F32, name="sums_t")
            add_windows(sums_t[k][:, 0:ROWS], a1[k])

        def turn_back(k):
            back[k] = sums_psum.tile([P, 2 * ROWS], F32, name="back")
            for b in range(2 * BLOCKS):
                cols = slice(b * P, (b + 1) * P)
                nc.tensor.transpose(out=back[k][:, cols], in_=yc_t[k][:, cols], identity=identity[:])

        def turn_grad_out():
            for half in range(2):
                g_ps = sums_psum.tile([P, CHUNKS * BLOCKS // 2, P], BF16, name="sums_t")
                for i in range(CHUNKS * BLOCKS // 2):
                    k, b = divmod(half * (CHUNKS * BLOCKS // 2) + i, BLOCKS)
                    rows = g_sb[:, k, :, :].rearrange("p j h -> p (j h)")
                    nc.tensor.transpose(out=g_ps[:, i, :], in_=rows[:, b * P : (b + 1) * P], identity=identity_bf[:])
                n = CHUNKS * BLOCKS // 2
                nc.scalar.copy(out=g_t[:, half * n : (half + 1) * n, :], in_=g_ps[:])

        def maximum(k):
            top[k] = two.tile([P, ROWS], F32, name="top")
            pieces = PACK if k == 0 else 1
            for i in range(pieces):
                rows = slice(i * ROWS // pieces, (i + 1) * ROWS // pieces)
                nc.vector.tensor_reduce(out=top[k][:, rows], in_=s_sb[k][:, rows, :], axis=AXIS.X, op=ALU.max, negate=True)

        def shift_on_tensor(k):
            r0 = ROWS - SHIFT_ON_TENSOR
            shifted[k] = shift_psum.tile([P, 2 * ROWS], F32, name="shifted")
            cells = shifted[k][:, 0 : SHIFT_ON_TENSOR * W]
            nc.tensor.matmul(out=cells, lhsT=identity[:], rhs=s_sb[k][:, r0:ROWS, :].rearrange("p r w -> p (r w)"), start=True, stop=False)
            nc.tensor.matmul(
                out=cells.rearrange("p (r w) -> p r w", w=W), lhsT=identity[:],
                rhs=top[k][:, r0:ROWS].unsqueeze(2).to_broadcast([P, SHIFT_ON_TENSOR, W]), start=False, stop=True,
            )

        def shift(k, engine, r0, r1):
            if k not in e:
                e[k] = four.tile(wide, F32, name="e")
            if r0 < r1:
                engine.tensor_tensor(
                    out=e[k][:, r0:r1, :], in0=s_sb[k][:, r0:r1, :],
                    in1=top[k][:, r0:r1].unsqueeze(2).to_broadcast([P, r1 - r0, W]), op=ALU.add,
                )

        def weigh_silu(k):
            nc.vector.scalar_tensor_tensor(
                out=a1[k][:], in0=a1[k][:], scalar=-1.0, in1=e[k][:], op0=ALU.add, op1=ALU.mult
            )

        def weigh_tanh(k):
            nc.vector.scalar_tensor_tensor(
                out=m1[k][:], in0=m1[k][:], scalar=3.0, in1=a1[k][:], op0=ALU.add, op1=ALU.mult
            )

        def mean(k):
            nc.vector.scalar_tensor_tensor(
                out=yc_t[k][:, ROWS : 2 * ROWS], in0=sums_t[k][:, 0:ROWS], scalar=-4.0, in1=guess[k],
                op0=ALU.mult, op1=ALU.mult,
            )

        def factor(k):
            yc_t[k] = three.tile([P, 2 * ROWS], F32, name="yc_t")
            nc.gpsimd.tensor_tensor(
                out=yc_t[k][:, 0:ROWS],
                in0=g_t[:, k * BLOCKS : (k + 1) * BLOCKS, :].rearrange("p b q -> p (b q)"),
                in1=guess[k], op=ALU.mult,
            )

        def weigh_mean(k, r0, r1, w0=0, w1=W):
            rows = slice(r0, r1)
            y2 = back[k][:, ROWS : 2 * ROWS]
            nc.vector.scalar_tensor_tensor(
                out=e[k][:, rows, w0:w1], in0=y2[:, rows].unsqueeze(2).to_broadcast([P, r1 - r0, w1 - w0]), scalar=2.0,
                in1=e[k][:, rows, w0:w1], op0=ALU.add, op1=ALU.mult,
            )

        def join(k, r0, r1, w0=0, w1=W):
            rows = slice(r0, r1)
            nc.gpsimd.tensor_tensor(out=m1[k][:, rows, w0:w1], in0=m1[k][:, rows, w0:w1], in1=e[k][:, rows, w0:w1], op=ALU.add)

        def join_on_tensor(k):
            joined[k] = z_psum.tile([P, 2 * ROWS], F32, name="z_t")
            cells = joined[k][:].rearrange("p (j x) -> p j x", j=PACK)
            for i, term in enumerate((m1[k], e[k])):
                part = term[:].rearrange("p (j h) w -> p j (h w)", j=PACK)[:, :, H_SPLIT * W :]
                nc.tensor.matmul(out=cells, lhsT=identity[:], rhs=part, start=(i == 0), stop=(i == 1))

        def keep_factor(k):
            c_sb[k] = two.tile([P, PACK, JOIN_FEATURES], F32, name="c_sb")
            nc.scalar.copy(out=c_sb[k][:], in_=back[k][:, 0:ROWS].rearrange("p (j h) -> p j h", j=PACK)[:, :, H_SPLIT:])

        def join_first_features(k, j0, j1):
            part = slice(0, H_SPLIT * W)
            m1_v = m1[k][:].rearrange("p (j h) w -> p j (h w)", j=PACK)[:, j0:j1, part]
            e_v = e[k][:].rearrange("p (j h) w -> p j (h w)", j=PACK)[:, j0:j1, part]
            nc.gpsimd.tensor_tensor(out=m1_v, in0=m1_v, in1=e_v, op=ALU.add)

        def write_ds(k, pieces=HALVES):
            tile_no = k // CHUNKS_PER_TILE
            if k % CHUNKS_PER_TILE == 0 and pieces[0][0] == 0:
                ds_grouped[tile_no] = two.tile([P, W, H_TILE, PACK], BF16, align_bytes=64, name="ds_grouped")
            f0 = (k % CHUNKS_PER_TILE) * H_CHUNK
            m1_v = m1[k][:].rearrange("p (j h) w -> p h j w", j=PACK)
            h1 = H_SPLIT if k in JOIN_ON_TENSOR else H_CHUNK
            if k in JOIN_ON_TENSOR:
                j_v = joined[k][:].rearrange("p (j h w) -> p h j w", j=PACK, w=W)
                for w0, w1 in pieces:
                    nc.vector.tensor_tensor(
                        out=ds_grouped[tile_no][:, w0:w1, f0 + h1 : f0 + H_CHUNK, :].rearrange("p w h j -> p h j w"),
                        in0=j_v[:, :, :, w0:w1],
                        in1=c_sb[k][:].rearrange("p j h -> p h j").unsqueeze(3).to_broadcast([P, JOIN_FEATURES, PACK, w1 - w0]),
                        op=ALU.mult,
                    )
            for w0, w1 in pieces:
                c_v = back[k][:, 0:ROWS].rearrange("p (j h) -> p h j", j=PACK)[:, 0:h1].unsqueeze(3).to_broadcast([P, h1, PACK, w1 - w0])
                nc.vector.tensor_tensor(
                    out=ds_grouped[tile_no][:, w0:w1, f0 : f0 + h1, :].rearrange("p w h j -> p h j w"),
                    in0=m1_v[:, 0:h1, :, w0:w1],
                    in1=c_v,
                    op=ALU.mult,
                )

        def quantise_ds(tile_no, w0, w1):
            if w0 == 0:
                ds_codes = two.tile([P, W, H_TILE], U32, align_bytes=64, name="ds_codes")
                ds_scales = two.tile([P, W, H_TILE], U8, align_bytes=64, name="ds_scales")
                quantised[tile_no] = (ds_codes, ds_scales)
            ds_codes, ds_scales = quantised[tile_no]
            nc.vector.quantize_mx(
                out=ds_codes[:, w0:w1, :].rearrange("p w h -> p (w h)").bitcast(E5M2_X4),
                scales=ds_scales[:, w0:w1, :].rearrange("p w h -> p (w h)"),
                in_=ds_grouped[tile_no][:, w0:w1, :, :].rearrange("p w h j -> p (w h j)"),
            )

        def regroup_x(w, copier):
            x_grouped[w] = three.tile([P, K, PACK], BF16, align_bytes=64, name="x_grouped")
            copier(
                out=x_grouped[w][:].rearrange("p (c i) j -> p c j i", i=8),
                in_=x_raw[w][:].rearrange("p j (c i) -> p c j i", i=8),
            )

        def quantise_x(w):
            nc.vector.quantize_mx(
                out=x_codes[:, w, :].bitcast(E4M3_X4),
                scales=x_scales[:, w, :],
                in_=x_grouped[w][:].rearrange("p c j -> p (c j)"),
            )

        accs = {}

        def products(tile_no, w0, w1, banks):
            ds_codes, ds_scales = quantised[tile_no]
            for w in range(w0, w1):
                pool, tag = banks[w % len(banks)]
                accs[w] = pool.tile([H_TILE, K], F32, name=tag)
                nc.tensor.matmul_mx(
                    out=accs[w][:],
                    lhsT=ds_codes[:, w, :].bitcast(E5M2_X4),
                    lhsT_scale=ds_scales[:, w, :],
                    rhs=x_codes[:, w, :].bitcast(E4M3_X4),
                    rhs_scale=x_scales[:, w, :],
                    start=True,
                    stop=True,
                )

        def empty_and_store(tile_no, w0, w1, copiers, single=False):
            rows = slice(tile_no * H_TILE, (tile_no + 1) * H_TILE)
            for w in range(w0, w1):
                i = w % STORE_BANKS
                if i == 0:
                    out_sb[0] = out_pool.tile([P, STORE_BANKS * K], F32, name="out_sb")
                copiers[w % len(copiers)](out=out_sb[0][:, i * K : (i + 1) * K], in_=accs[w][:])
                if single:
                    nc.sync.dma_start(out=out[rows, w * K : (w + 1) * K], in_=out_sb[0][:, i * K : (i + 1) * K])
                elif i == STORE_BANKS - 1:
                    first = (w - i) * K
                    nc.sync.dma_start(out=out[rows, first : first + STORE_BANKS * K], in_=out_sb[0][:])

        late = []
        pend = []
        banks = [(acc_psum, "acc")] * ACC_BANKS
        LAST = H // H_TILE - 1
        for r in range(CHUNKS + 4):
            def stage(lag):
                return r - lag if 0 <= r - lag < CHUNKS else None

            new, mid, mk, yk, wk = stage(0), stage(1), stage(3), stage(4), stage(5)
            windows = list(X_PLAN[r]) if r < len(X_PLAN) else []
            if r == 0:
                load_s(0)
            if r + 1 < CHUNKS:
                load_s(r + 1)
            if r == 0:
                load_x(0)
            for w in windows:
                if w > 0:
                    load_x(w)
            if r == 0:
                for j in range(PACK):
                    nc.sync.dma_start(out=g_sb[:, :, j, :], in_=g_rows[:, j, :].rearrange("p (k h) -> p k h", h=H_CHUNK))

            if r % 2 == 0 and r < CHUNKS:
                if mid is not None:
                    silu(mid)
                silu(new)

            pair_due = r % 2 == 1 and 3 <= r <= CHUNKS + 1
            if pair_due and yk is None:
                factor(r - 3)
            if yk in JOIN_ON_TENSOR:
                weigh_mean(yk, 0, H_CHUNK)
                join_first_features(yk, 0, 1)
                if pair_due:
                    factor(r - 3)
                weigh_mean(yk, H_CHUNK, ROWS)
                keep_factor(yk)
                join_on_tensor(yk)
                join_first_features(yk, 1, PACK)
            elif yk is not None and yk != CHUNKS - 1:
                weigh_mean(yk, 0, FIRST)
                join(yk, 0, FIRST)
                if pair_due:
                    factor(r - 3)
                weigh_mean(yk, FIRST, ROWS)
                join(yk, FIRST, ROWS)
            if pair_due:
                factor(r - 2)
            share = SHIFT_ON_GPSIMD if r >= 5 else 0
            if new is not None:
                maximum(new)
                tens = SHIFT_ON_TENSOR if new >= TFROM else 0
                if tens:
                    shift_on_tensor(new)
                shift(new, nc.gpsimd, ROWS - tens - share, ROWS - tens)
            if wk is not None and wk < CHUNKS - 2:
                write_ds(wk)
            if mk is not None and r > 3:
                mean(mk)
                turn_back(mk)

            shift_first = r in (1, 3)
            if new is not None and shift_first:
                shift(new, nc.vector, 0, ROWS - tens - share)
            if mid is not None:
                weigh_silu(mid)
            if new is not None and not shift_first:
                shift(new, nc.vector, 0, ROWS - tens - share)
            if mk is not None and r == 3:
                mean(mk)
                turn_back(mk)
            if r == CHUNKS:
                banks.append((shift_psum, "shifted"))
            if yk == CHUNKS - 1:
                banks += [(z_psum, "z_t")] + [(sums_psum, "sums_t")] * 2 + [(sums_psum, "back")] * 2
            todo, pend = (pend, []) if r != 7 else ([], pend)
            if wk is not None and wk % 2 == 1:
                todo.append((wk // 2, 0, 4))
                (todo if r > CHUNKS else pend).append((wk // 2, 4, 8))
            if wk is not None and wk % 2 == 1:
                quantise_ds(wk // 2, 0, W)
            if mid is not None and not (r == 1):
                add_y(mid)
            for w in late:
                quantise_x(w)
            late = list(windows)
            for w in windows:
                if w not in X_ON_SCALAR:
                    regroup_x(w, nc.vector.tensor_copy)
            if r == 0:
                quantise_x(late.pop(0))
            if mid is not None:
                weigh_tanh(mid)
            if r % 2 == 0 and 2 <= r <= CHUNKS:
                guess_reciprocals(r - 2)
            if new is not None:
                tanh(new)
                exponential(new)
                if new == CHUNKS - 1:
                    silu(new)
            if r == 0:
                turn_grad_out()
            if r == 1:
                add_z(new)
                add_y(mid)
            for tile_no, w0, w1 in todo:
                products(tile_no, w0, w1, banks)
                empty_and_store(tile_no, w0, w1, [nc.scalar.copy])
            if new is not None and not (r == 1):
                add_z(new)
            for w in windows:
                if w in X_ON_SCALAR:
                    regroup_x(w, nc.scalar.copy)
            if yk == CHUNKS - 1:
                for w0, w1 in HALVES:
                    weigh_mean(yk, 0, ROWS, w0, w1)
                    join(yk, 0, ROWS, w0, w1)
                write_ds(yk - 1, HALVES[:1])
                write_ds(yk, HALVES[:1])
                write_ds(yk - 1, HALVES[1:])
                for w0, w1 in HALVES:
                    if w0 > 0:
                        write_ds(yk, HALVES[1:])
                    quantise_ds(LAST, w0, w1)
                    products(LAST, w0, w1, banks)
                    empty_and_store(LAST, w0, w1, [nc.scalar.copy] if w0 == 0 else [nc.vector.tensor_copy, nc.scalar.copy], True)
